import numpy as np
import ml_dtypes


def mxq(x, axis, fmt="e4m3"):
    dtype, down = {"e4m3": (ml_dtypes.float8_e4m3fn, 7), "e5m2": (ml_dtypes.float8_e5m2, 14)}[fmt]
    v = np.moveaxis(np.asarray(x, np.float32).astype(ml_dtypes.bfloat16).astype(np.float64), axis, -1)
    blocks = v.reshape(v.shape[:-1] + (-1, 32))
    amax = np.abs(blocks).max(-1, keepdims=True)
    byte = np.maximum(np.where(amax > 0, np.frexp(amax)[1] - 1 + 127, 0) - down, 1)
    scale = np.exp2(byte - 127.0)
    codes = (blocks / scale).astype(np.float32).astype(dtype).astype(np.float64)
    return np.moveaxis((codes * scale).reshape(v.shape), -1, axis)


WIDE = False


def mx_kscale(k):
    if not WIDE:
        return np.ones(k)
    levels = np.array([10, -10, 5, -5, 0])
    a = np.random.permutation(np.resize(levels, k // 512 * 4)).reshape(k // 512, 4)
    idx = np.arange(k)
    return np.exp2(a[idx // 512, idx % 128 // 32])


BF16 = ml_dtypes.bfloat16


def bf(x):
    return np.asarray(x, np.float32).astype(BF16)


def f64(x):
    return np.asarray(x).astype(np.float64)


N, IN, OUT, R, KD, K = 4096, 1024, 256, 32, 32, 16
KR = K * R
GATE_THRESHOLD = 0.05


def setup_inputs():
    s, t = mx_kscale(IN), mx_kscale(KR)
    tk = t.reshape(K, R)
    return {"x": bf(np.random.standard_normal((N, IN)) * s),
            "scores": bf(np.random.standard_normal((N, K))),
            "Wb": bf(np.random.standard_normal((OUT, IN)) / np.sqrt(IN) / s),
            "bb": bf(np.random.standard_normal(OUT) * 0.3),
            "A": bf(np.random.standard_normal((K, OUT, R)) * 2.0 / np.sqrt(R) / tk[:, None, :]),
            "B": bf(np.random.standard_normal((K, R, IN)) / np.sqrt(IN) / s * tk[:, :, None])}


def reference(x, scores, Wb, bb, A, B):
    xq = mxq(f64(x), 1, "e4m3")
    base = (xq @ mxq(f64(Wb), 1, "e4m3").T) + f64(bb)
    sc = f64(scores)
    e = np.exp(sc - sc.max(-1, keepdims=True))
    g = e / e.sum(-1, keepdims=True)
    g = np.where(g > GATE_THRESHOLD, g, 0.0)
    g = g / np.maximum(g.sum(-1, keepdims=True), 1e-8)
    u = xq @ mxq(f64(B).reshape(KR, IN), 1, "e4m3").T
    h = (g[:, :, None] * u.reshape(N, K, R)).reshape(N, KR)
    Af = f64(A).transpose(0, 2, 1).reshape(KR, OUT)
    delta = mxq(h, 1, "e4m3") @ mxq(Af, 0, "e4m3")
    return base + delta

@@ -1,0 +1,350 @@
+from contextlib import ExitStack
+
+import concourse.mybir as mybir
+from concourse.masks import make_identity
+
+F32 = mybir.dt.float32
+BF16 = mybir.dt.bfloat16
+U32 = mybir.dt.uint32
+U8 = mybir.dt.uint8
+FP8X4 = mybir.dt.float8_e4m3fn_x4
+ALU = mybir.AluOpType
+ACT = mybir.ActivationFunctionType
+AX = mybir.AxisListType
+
+P = 128
+NT = 32
+FLOPS = 2 * 4096 * 1024 * 768 + 2 * 4096 * 512 * 256
+
+MANUAL = True
+GROUPS = [(0, 2), (2, 2), (4, 2), (6, 2), (8, 4), (12, 4), (16, 4), (20, 4), (24, 4), (28, 2), (30, 1), (31, 1)]
+E_ON_DVE_FROM = 9
+GATE_PARTS = [(0, 8), (8, 32)]
+
+
+def tile_submatrixlinear_pa_t_kernel(tc, x, scores, Wb, bb, A, B, out):
+    nc = tc.nc
+    ng = len(GROUPS)
+    with ExitStack() as ctx:
+        const = ctx.enter_context(tc.tile_pool(name="const", bufs=1))
+        xin_pool = ctx.enter_context(tc.tile_pool(name="xin", bufs=1))
+        xg_pool = ctx.enter_context(tc.tile_pool(name="xg", bufs=3))
+        xq_pool = ctx.enter_context(tc.tile_pool(name="xq", bufs=4))
+        h_pool = ctx.enter_context(tc.tile_pool(name="h", bufs=2))
+        hq_pool = ctx.enter_context(tc.tile_pool(name="hq", bufs=3))
+        ob_pool = ctx.enter_context(tc.tile_pool(name="ob", bufs=3))
+        psum = ctx.enter_context(tc.psum_pool(name="psum", bufs=1))
+        if MANUAL:
+            ctx.enter_context(tc.manual_schedule())
+
+        rot = {"tp": [0, 1, 2], "u": [3, 4, 5], "o": [6, 7]}
+        cnt_rot = {"tp": 0, "u": 0, "o": 0}
+
+        def bank(kind):
+            b = rot[kind][cnt_rot[kind] % len(rot[kind])]
+            cnt_rot[kind] = cnt_rot[kind] + 1
+            return psum.tile([P, 512], F32, name="bank%d" % b, tag="bank%d" % b)
+
+        ident = const.tile([P, P], F32, name="ident")
+        ones = const.tile([P, P], BF16, name="ones")
+        bbz = const.tile([P, 256], BF16, name="bbz")
+        bb2 = const.tile([P, 512], F32, name="bb2")
+        warm = const.tile([P, 1], F32, name="warm")
+        sc = const.tile([P, 512], BF16, name="sc")
+        gexp = const.tile([P, NT * P], F32, name="gexp")
+        gT = const.tile([P, NT * P], F32, name="gT")
+        Bsb = const.tile([P, 4096], BF16, name="Bsb")
+        Wsb = const.tile([P, 2048], BF16, name="Wsb")
+        Asb = const.tile([P, 1024], BF16, name="Asb")
+        Bq = const.tile([P, 1024], U32, name="Bq", align_bytes=64)
+        Bs = const.tile([P, 1024], U8, name="Bs", align_bytes=64)
+        Wq = const.tile([P, 512], U32, name="Wq", align_bytes=64)
+        Ws = const.tile([P, 512], U8, name="Ws", align_bytes=64)
+        Aq = const.tile([P, 256], U32, name="Aq", align_bytes=64)
+        As = const.tile([P, 256], U8, name="As", align_bytes=64)
+        xin = [xin_pool.tile([P, 4096], BF16, name="xin%d" % i) for i in range(8)]
+
+        nc.vector.memset(warm[:], 0.0)
+        nc.vector.memset(bbz[:], 0.0)
+        nc.vector.memset(ones[:], 1.0)
+        make_identity(nc, ident[:])
+        nc.scalar.activation(out=warm[:], in_=warm[:], func=ACT.Exp)
+
+        x_v = x.rearrange("(p t) i -> p t i", t=NT)
+        out_v = out.rearrange("(p t) o -> p t o", t=NT)
+        B_v = B.rearrange("k r i -> (k r) i").rearrange("(p j) i -> p j i", j=4)
+
+        def load_x(t0, cnt):
+            dst = xin[t0 // 4][:, (t0 % 4) * 1024 : (t0 % 4 + cnt) * 1024]
+            nc.sync.dma_start(out=dst.rearrange("p (t i) -> p t i", i=1024), in_=x_v[:, t0 : t0 + cnt, :])
+
+        nc.sync.dma_start(out=sc[:].rearrange("p (t k) -> p t k", k=16), in_=scores.rearrange("(p t) k -> p t k", t=NT))
+        load_x(0, 2)
+        for j in range(4):
+            nc.sync.dma_start(out=Bsb[:, j * 1024 : (j + 1) * 1024], in_=B_v[:, j, :])
+        load_x(2, 2)
+        nc.sync.dma_start(out=Wsb[:].rearrange("p (h i) -> p h i", h=2), in_=Wb.rearrange("(h p) i -> p h i", p=P))
+        for h in range(2):
+            nc.sync.dma_start(
+                out=Asb[:, h * 512 : (h + 1) * 512].rearrange("p (k r) -> p k r", r=32),
+                in_=A[:, h * P : (h + 1) * P, :].rearrange("k p r -> p k r"),
+            )
+        nc.sync.dma_start(out=bbz[0:1, :], in_=bb.rearrange("(o n) -> o n", o=1))
+        load_x(4, 2)
+        load_x(6, 2)
+        for i in range(2, 8):
+            load_x(4 * i, 4)
+
+        def t_rowtile(bk, src32, col0):
+            for c in range(4):
+                nc.tensor.transpose(bk[:, c * P : (c + 1) * P], src32[:, col0 + c * P : col0 + (c + 1) * P], ident[:])
+
+        def c_rowtile(bk, dst):
+            nc.scalar.copy(out=dst, in_=bk[:].rearrange("p (g u n) -> p g n u", g=2, u=2))
+
+        def gate_steps(part, ta, tb, on_pool):
+            n = tb - ta
+            w = n * 16
+            s3 = sc[:, ta * 16 : tb * 16].rearrange("p (t k) -> p t k", k=16)
+            mx = const.tile([P, n], F32, name="mx%d" % part)
+            dd = const.tile([P, w], F32, name="dd%d" % part)
+            ee = const.tile([P, w], F32, name="ee%d" % part)
+            ss = const.tile([P, n], F32, name="ss%d" % part)
+            rs = const.tile([P, n], F32, name="rs%d" % part)
+            g0 = const.tile([P, w], F32, name="g0%d" % part)
+            g1 = const.tile([P, w], F32, name="g1%d" % part)
+            s1 = const.tile([P, n], F32, name="s1%d" % part)
+            r1 = const.tile([P, n], F32, name="r1%d" % part)
+            gg = const.tile([P, w], F32, name="gg%d" % part)
+            el = nc.gpsimd if on_pool else nc.vector
+
+            def v3(t):
+                return t[:].rearrange("p (t k) -> p t k", k=16)
+
+            def b3(t):
+                return t[:].unsqueeze(2).to_broadcast([P, n, 16])
+
+            def st_max():
+                nc.vector.tensor_reduce(out=mx[:], in_=s3, axis=AX.X, op=ALU.max)
+
+            def st_sub():
+                el.tensor_tensor(out=v3(dd), in0=s3, in1=b3(mx), op=ALU.subtract)
+
+            def st_exp():
+                nc.scalar.activation(out=ee[:], in_=dd[:], func=ACT.Exp)
+
+            def st_sum():
+                nc.vector.tensor_reduce(out=ss[:], in_=v3(ee), axis=AX.X, op=ALU.add)
+                nc.vector.reciprocal(out=rs[:], in_=ss[:])
+
+            def st_g0():
+                el.tensor_tensor(out=v3(g0), in0=v3(ee), in1=b3(rs), op=ALU.mult)
+
+            def st_thr():
+                if on_pool:
+                    mk = const.tile([P, w], F32, name="mk%d" % part)
+                    nc.gpsimd.tensor_scalar(out=mk[:], in0=g0[:], scalar1=0.05, scalar2=1.0, op0=ALU.is_gt, op1=ALU.mult)
+                    nc.gpsimd.tensor_tensor(out=g1[:], in0=mk[:], in1=g0[:], op=ALU.mult)
+                else:
+                    nc.vector.scalar_tensor_tensor(out=g1[:], in0=g0[:], scalar=0.05, in1=g0[:], op0=ALU.is_gt, op1=ALU.mult)
+
+            def st_sum1():
+                nc.vector.tensor_reduce(out=s1[:], in_=v3(g1), axis=AX.X, op=ALU.add)
+                nc.vector.tensor_scalar_max(out=s1[:], in0=s1[:], scalar1=1e-8)
+                nc.vector.reciprocal(out=r1[:], in_=s1[:])
+
+            def st_g():
+                el.tensor_tensor(out=v3(gg), in0=v3(g1), in1=b3(r1), op=ALU.mult)
+
+            def st_expand(c0):
+                def f():
+                    nc.gpsimd.tensor_scalar(
+                        out=gexp[:, (ta + c0) * P : (ta + c0 + 4) * P].rearrange("p (c r) -> p c r", r=8),
+                        in0=gg[:, c0 * 16 : (c0 + 4) * 16].unsqueeze(2).to_broadcast([P, 64, 8]),
+                        scalar1=1.0, scalar2=0.0, op0=ALU.mult, op1=ALU.add,
+                    )
+                return f
+
+            return [st_max, st_sub, st_exp, st_sum, st_g0, st_thr, st_sum1, st_g] + [st_expand(c0) for c0 in range(0, n, 4)]
+
+        xgs = {}
+        xqs = {}
+        hgs = {}
+        hqs = {}
+
+        def emit_T(k):
+            t0, cnt = GROUPS[k]
+            xg = xg_pool.tile([P, 4096], BF16, name="xg", tag="xg", align_bytes=64)
+            xg32 = xg[:].bitcast(F32)
+            for tt in range(cnt):
+                t = t0 + tt
+                bk = bank("tp")
+                t_rowtile(bk, xin[t // 4][:].bitcast(F32), (t % 4) * 512)
+                c_rowtile(bk, xg32[:, tt * 512 : (tt + 1) * 512].rearrange("p (g n u) -> p g n u", g=2, u=2))
+            xgs[k] = xg
+
+        def emit_Tg(k):
+            t0, cnt = GROUPS[k]
+            bk = bank("tp")
+            for tt in range(cnt):
+                t = t0 + tt
+                nc.tensor.transpose(bk[:, tt * P : (tt + 1) * P], gexp[:, t * P : (t + 1) * P], ident[:])
+            nc.scalar.copy(out=gT[:, t0 * P : (t0 + cnt) * P], in_=bk[:, 0 : cnt * P])
+
+        def emit_Q(k):
+            t0, cnt = GROUPS[k]
+            xq = xq_pool.tile([P, 1024], U32, name="xq", tag="xq", align_bytes=64)
+            xs = xq_pool.tile([P, 1024], U8, name="xs", tag="xs", align_bytes=64)
+            nc.vector.quantize_mx(
+                out=xq[:, 0 : cnt * 256].bitcast(FP8X4), scales=xs[:, 0 : cnt * 256], in_=xgs[k][:, 0 : cnt * 1024]
+            )
+            xqs[k] = (xq, xs)
+
+        def emit_U(k):
+            t0, cnt = GROUPS[k]
+            xq, xs = xqs[k]
+            hg = h_pool.tile([P, 2048], BF16, name="hg", tag="hg", align_bytes=64)
+            for tt in range(cnt):
+                t = t0 + tt
+                bk = bank("u")
+                for j in range(4):
+                    for g in range(2):
+                        wc = slice((j * 2 + g) * P, (j * 2 + g + 1) * P)
+                        xc = slice((tt * 2 + g) * P, (tt * 2 + g + 1) * P)
+                        nc.tensor.matmul_mx(
+                            out=bk[:, j * P : (j + 1) * P],
+                            lhsT=Bq[:, wc].bitcast(FP8X4), lhsT_scale=Bs[:, wc],
+                            rhs=xq[:, xc].bitcast(FP8X4), rhs_scale=xs[:, xc],
+                            start=(g == 0), stop=(g == 1),
+                        )
+                nc.vector.tensor_tensor(
+                    out=hg[:, tt * 512 : (tt + 1) * 512].rearrange("p (n j) -> p n j", j=4),
+                    in0=bk[:].rearrange("p (j n) -> p n j", j=4),
+                    in1=gT[:, t * P : (t + 1) * P].unsqueeze(2).to_broadcast([P, P, 4]),
+                    op=ALU.mult,
+                )
+            hgs[k] = hg
+
+        def emit_Hq(k):
+            t0, cnt = GROUPS[k]
+            hq = hq_pool.tile([P, 512], U32, name="hq", tag="hq", align_bytes=64)
+            hs = hq_pool.tile([P, 512], U8, name="hs", tag="hs", align_bytes=64)
+            nc.vector.quantize_mx(
+                out=hq[:, 0 : cnt * P].bitcast(FP8X4), scales=hs[:, 0 : cnt * P], in_=hgs[k][:, 0 : cnt * 512]
+            )
+            hqs[k] = (hq, hs)
+
+        def emit_O(k):
+            t0, cnt = GROUPS[k]
+            xq, xs = xqs[k]
+            hq, hs = hqs[k]
+            ob = ob_pool.tile([P, 1024], F32, name="ob", tag="ob")
+            for p0 in range(0, cnt, 2):
+                np_ = min(2, cnt - p0)
+                bk = bank("o")
+                for q in range(np_):
+                    tt = p0 + q
+                    oc = slice(q * 256, (q + 1) * 256)
+                    for g in range(2):
+                        xc = slice((tt * 2 + g) * P, (tt * 2 + g + 1) * P)
+                        nc.tensor.matmul_mx(
+                            out=bk[:, oc],
+                            lhsT=xq[:, xc].bitcast(FP8X4), lhsT_scale=xs[:, xc],
+                            rhs=Wq[:, g * 256 : (g + 1) * 256].bitcast(FP8X4), rhs_scale=Ws[:, g * 256 : (g + 1) * 256],
+                            start=(g == 0), stop=False,
+                        )
+                    hc = slice(tt * P, (tt + 1) * P)
+                    nc.tensor.matmul_mx(
+                        out=bk[:, oc],
+                        lhsT=hq[:, hc].bitcast(FP8X4), lhsT_scale=hs[:, hc],
+                        rhs=Aq[:].bitcast(FP8X4), rhs_scale=As[:],
+                        start=False, stop=True,
+                    )
+                w = np_ * 256
+                dst = ob[:, p0 * 256 : p0 * 256 + w]
+                if k >= E_ON_DVE_FROM:
+                    nc.vector.tensor_tensor(out=dst, in0=bk[:, 0:w], in1=bb2[:, 0:w], op=ALU.add)
+                else:
+                    nc.scalar.copy(out=dst, in_=bk[:, 0:w])
+                    nc.gpsimd.tensor_tensor(out=dst, in0=dst, in1=bb2[:, 0:w], op=ALU.add)
+            nc.sync.dma_start(out=out_v[:, t0 : t0 + cnt, :], in_=ob[:, 0 : cnt * 256].rearrange("p (t o) -> p t o", o=256))
+
+        steps1 = gate_steps(0, GATE_PARTS[0][0], GATE_PARTS[0][1], False)
+        steps2 = gate_steps(1, GATE_PARTS[1][0], GATE_PARTS[1][1], True)
+        steps2[0]()
+        steps2[1]()
+        for f in steps1[0:3]:
+            f()
+        steps2[2]()
+        for f in steps1[3:]:
+            f()
+        emit_T(0)
+        Bg = xg_pool.tile([P, 4096], BF16, name="Bg", tag="xg", align_bytes=64)
+        Bg32 = Bg[:].bitcast(F32)
+        Bsb32 = Bsb[:].bitcast(F32)
+        for j in range(4):
+            bk = bank("u" if j < 3 else "o")
+            t_rowtile(bk, Bsb32, j * 512)
+            c_rowtile(bk, Bg32[:, j * 512 : (j + 1) * 512].rearrange("p (g n u) -> p g n u", g=2, u=2))
+        emit_Q(0)
+        for hf in range(2):
+            nc.vector.quantize_mx(
+                out=Bq[:, hf * 512 : (hf + 1) * 512].bitcast(FP8X4),
+                scales=Bs[:, hf * 512 : (hf + 1) * 512],
+                in_=Bg[:, hf * 2048 : (hf + 1) * 2048],
+            )
+        emit_Tg(0)
+        steps2[3]()
+        steps2[4]()
+        steps2[5]()
+
+        def prep_WA():
+            WAg = xg_pool.tile([P, 4096], BF16, name="WAg", tag="xg", align_bytes=64)
+            WAg32 = WAg[:].bitcast(F32)
+            Wsb32 = Wsb[:].bitcast(F32)
+            for h in range(2):
+                bk = bank("o")
+                t_rowtile(bk, Wsb32, h * 512)
+                c_rowtile(bk, WAg32[:, 0:1024].rearrange("p (g h n u) -> p g h n u", g=2, h=2, u=2)[:, :, h])
+            bk = bank("tp")
+            A4 = Asb[:].bitcast(F32).rearrange("p (h m u) -> p h m u", h=2, u=2)
+            for u in range(2):
+                for h in range(2):
+                    nc.tensor.transpose(bk[:, u * 256 + h * P : u * 256 + (h + 1) * P], A4[:, h, :, u], ident[:])
+            nc.scalar.copy(
+                out=WAg32[:, 1024:1536].rearrange("p (o u) -> p o u", u=2),
+                in_=bk[:].rearrange("p (u o) -> p o u", u=2),
+            )
+            bk = bank("tp")
+            nc.tensor.matmul(out=bk[:, 0:256], lhsT=ones[:], rhs=bbz[:], start=True, stop=True)
+            nc.scalar.copy(
+                out=bb2[:].rearrange("p (r o) -> p r o", r=2),
+                in_=bk[:, 0:256].unsqueeze(1).to_broadcast([P, 2, 256]),
+            )
+            return WAg
+
+        def quant_WA(WAg):
+            nc.vector.quantize_mx(out=Wq[:].bitcast(FP8X4), scales=Ws[:], in_=WAg[:, 0:2048])
+            nc.vector.quantize_mx(out=Aq[:].bitcast(FP8X4), scales=As[:], in_=WAg[:, 2048:3072])
+
+        rest2 = steps2[6:]
+        for i in range(-1, ng):
+            if i + 2 < ng:
+                emit_T(i + 2)
+                emit_Tg(i + 2)
+            if i + 1 < ng:
+                emit_U(i + 1)
+            if i + 2 < ng:
+                emit_Q(i + 2)
+            if i == -1:
+                for f in rest2[0:4]:
+                    f()
+            if i == 0:
+                for f in rest2[4:]:
+                    f()
+            if i + 1 < ng:
+                emit_Hq(i + 1)
+            if i == -1:
+                quant_WA(prep_WA())
+            if i >= 0:
+                emit_O(i)

@@ -18,7 +18,7 @@ FLOPS = 2 * 4096 * 1024 * 768 + 2 * 4096 * 512 * 256
 
 MANUAL = True
 GROUPS = [(0, 2), (2, 2), (4, 2), (6, 2), (8, 4), (12, 4), (16, 4), (20, 4), (24, 4), (28, 2), (30, 1), (31, 1)]
-E_ON_DVE_FROM = 9
+E_ON_DVE_FROM = 0
 GATE_PARTS = [(0, 8), (8, 32)]
 
 

@@ -18,7 +18,7 @@ FLOPS = 2 * 4096 * 1024 * 768 + 2 * 4096 * 512 * 256
 
 MANUAL = True
 GROUPS = [(0, 2), (2, 2), (4, 2), (6, 2), (8, 4), (12, 4), (16, 4), (20, 4), (24, 4), (28, 2), (30, 1), (31, 1)]
-E_ON_DVE_FROM = 0
+E_ON_DVE_FROM = 9
 GATE_PARTS = [(0, 8), (8, 32)]
 
 
@@ -37,7 +37,7 @@ def tile_submatrixlinear_pa_t_kernel(tc, x, scores, Wb, bb, A, B, out):
         if MANUAL:
             ctx.enter_context(tc.manual_schedule())
 
-        rot = {"tp": [0, 1, 2], "u": [3, 4, 5], "o": [6, 7]}
+        rot = {"tp": [0, 1, 2, 3, 4], "u": [5, 6], "o": [7]}
         cnt_rot = {"tp": 0, "u": 0, "o": 0}
 
         def bank(kind):
@@ -171,6 +171,7 @@ def tile_submatrixlinear_pa_t_kernel(tc, x, scores, Wb, bb, A, B, out):
         xqs = {}
         hgs = {}
         hqs = {}
+        obs = {}
 
         def emit_T(k):
             t0, cnt = GROUPS[k]
@@ -200,11 +201,13 @@ def tile_submatrixlinear_pa_t_kernel(tc, x, scores, Wb, bb, A, B, out):
             )
             xqs[k] = (xq, xs)
 
-        def emit_U(k):
+        def emit_U(k, p0):
             t0, cnt = GROUPS[k]
             xq, xs = xqs[k]
-            hg = h_pool.tile([P, 2048], BF16, name="hg", tag="hg", align_bytes=64)
-            for tt in range(cnt):
+            if p0 == 0:
+                hgs[k] = h_pool.tile([P, 2048], BF16, name="hg", tag="hg", align_bytes=64)
+            hg = hgs[k]
+            for tt in range(p0, min(p0 + 2, cnt)):
                 t = t0 + tt
                 bk = bank("u")
                 for j in range(4):
@@ -223,7 +226,6 @@ def tile_submatrixlinear_pa_t_kernel(tc, x, scores, Wb, bb, A, B, out):
                     in1=gT[:, t * P : (t + 1) * P].unsqueeze(2).to_broadcast([P, P, 4]),
                     op=ALU.mult,
                 )
-            hgs[k] = hg
 
         def emit_Hq(k):
             t0, cnt = GROUPS[k]
@@ -234,12 +236,14 @@ def tile_submatrixlinear_pa_t_kernel(tc, x, scores, Wb, bb, A, B, out):
             )
             hqs[k] = (hq, hs)
 
-        def emit_O(k):
+        def emit_O(k, p0):
             t0, cnt = GROUPS[k]
             xq, xs = xqs[k]
             hq, hs = hqs[k]
-            ob = ob_pool.tile([P, 1024], F32, name="ob", tag="ob")
-            for p0 in range(0, cnt, 2):
+            if p0 == 0:
+                obs[k] = ob_pool.tile([P, 1024], F32, name="ob", tag="ob")
+            ob = obs[k]
+            if True:
                 np_ = min(2, cnt - p0)
                 bk = bank("o")
                 for q in range(np_):
@@ -267,7 +271,8 @@ def tile_submatrixlinear_pa_t_kernel(tc, x, scores, Wb, bb, A, B, out):
                 else:
                     nc.scalar.copy(out=dst, in_=bk[:, 0:w])
                     nc.gpsimd.tensor_tensor(out=dst, in0=dst, in1=bb2[:, 0:w], op=ALU.add)
-            nc.sync.dma_start(out=out_v[:, t0 : t0 + cnt, :], in_=ob[:, 0 : cnt * 256].rearrange("p (t o) -> p t o", o=256))
+            if p0 + 2 >= cnt:
+                nc.sync.dma_start(out=out_v[:, t0 : t0 + cnt, :], in_=ob[:, 0 : cnt * 256].rearrange("p (t o) -> p t o", o=256))
 
         steps1 = gate_steps(0, GATE_PARTS[0][0], GATE_PARTS[0][1], False)
         steps2 = gate_steps(1, GATE_PARTS[1][0], GATE_PARTS[1][1], True)
@@ -283,7 +288,7 @@ def tile_submatrixlinear_pa_t_kernel(tc, x, scores, Wb, bb, A, B, out):
         Bg32 = Bg[:].bitcast(F32)
         Bsb32 = Bsb[:].bitcast(F32)
         for j in range(4):
-            bk = bank("u" if j < 3 else "o")
+            bk = bank("tp")
             t_rowtile(bk, Bsb32, j * 512)
             c_rowtile(bk, Bg32[:, j * 512 : (j + 1) * 512].rearrange("p (g n u) -> p g n u", g=2, u=2))
         emit_Q(0)
@@ -303,7 +308,7 @@ def tile_submatrixlinear_pa_t_kernel(tc, x, scores, Wb, bb, A, B, out):
             WAg32 = WAg[:].bitcast(F32)
             Wsb32 = Wsb[:].bitcast(F32)
             for h in range(2):
-                bk = bank("o")
+                bk = bank("tp")
                 t_rowtile(bk, Wsb32, h * 512)
                 c_rowtile(bk, WAg32[:, 0:1024].rearrange("p (g h n u) -> p g h n u", g=2, h=2, u=2)[:, :, h])
             bk = bank("tp")
@@ -332,8 +337,13 @@ def tile_submatrixlinear_pa_t_kernel(tc, x, scores, Wb, bb, A, B, out):
             if i + 2 < ng:
                 emit_T(i + 2)
                 emit_Tg(i + 2)
-            if i + 1 < ng:
-                emit_U(i + 1)
+            nu = GROUPS[i + 1][1] if i + 1 < ng else 0
+            no = GROUPS[i][1] if i >= 0 else 0
+            for p0 in range(0, max(nu, no), 2):
+                if p0 < nu:
+                    emit_U(i + 1, p0)
+                if p0 < no:
+                    emit_O(i, p0)
             if i + 2 < ng:
                 emit_Q(i + 2)
             if i == -1:
@@ -346,5 +356,3 @@ def tile_submatrixlinear_pa_t_kernel(tc, x, scores, Wb, bb, A, B, out):
                 emit_Hq(i + 1)
             if i == -1:
                 quant_WA(prep_WA())
-            if i >= 0:
-                emit_O(i)

@@ -17,9 +17,16 @@ NT = 32
 FLOPS = 2 * 4096 * 1024 * 768 + 2 * 4096 * 512 * 256
 
 MANUAL = True
-GROUPS = [(0, 2), (2, 2), (4, 2), (6, 2), (8, 4), (12, 4), (16, 4), (20, 4), (24, 4), (28, 2), (30, 1), (31, 1)]
-E_ON_DVE_FROM = 9
+GROUPS = [(0, 2), (2, 2), (4, 2), (6, 2), (8, 4), (12, 4), (16, 4), (20, 4), (24, 4), (28, 2), (30, 2)]
+E_ON_DVE_FROM = 7
 GATE_PARTS = [(0, 8), (8, 32)]
+LT = 2
+LO = 3
+V3_AT = 0
+PREP_WA_AT = 2
+LATE_LOADS = {2: 7}
+LOADS = ["sc", (0, 2), "B", (2, 2), (4, 2), (6, 2), "W", "bb", (8, 4), "A", (12, 4), (16, 4), (20, 4), (24, 4)]
+LG = 1
 
 
 def tile_submatrixlinear_pa_t_kernel(tc, x, scores, Wb, bb, A, B, out):
@@ -29,15 +36,15 @@ def tile_submatrixlinear_pa_t_kernel(tc, x, scores, Wb, bb, A, B, out):
         const = ctx.enter_context(tc.tile_pool(name="const", bufs=1))
         xin_pool = ctx.enter_context(tc.tile_pool(name="xin", bufs=1))
         xg_pool = ctx.enter_context(tc.tile_pool(name="xg", bufs=3))
-        xq_pool = ctx.enter_context(tc.tile_pool(name="xq", bufs=4))
+        xq_pool = ctx.enter_context(tc.tile_pool(name="xq", bufs=LT + LO + 1))
         h_pool = ctx.enter_context(tc.tile_pool(name="h", bufs=2))
-        hq_pool = ctx.enter_context(tc.tile_pool(name="hq", bufs=3))
+        hq_pool = ctx.enter_context(tc.tile_pool(name="hq", bufs=LO + 2))
         ob_pool = ctx.enter_context(tc.tile_pool(name="ob", bufs=3))
         psum = ctx.enter_context(tc.psum_pool(name="psum", bufs=1))
         if MANUAL:
             ctx.enter_context(tc.manual_schedule())
 
-        rot = {"tp": [0, 1, 2, 3, 4], "u": [5, 6], "o": [7]}
+        rot = {"tp": [0, 1, 2, 3], "u": [4, 5], "o": [6, 7]}
         cnt_rot = {"tp": 0, "u": 0, "o": 0}
 
         def bank(kind):
@@ -51,18 +58,20 @@ def tile_submatrixlinear_pa_t_kernel(tc, x, scores, Wb, bb, A, B, out):
         bb2 = const.tile([P, 512], F32, name="bb2")
         warm = const.tile([P, 1], F32, name="warm")
         sc = const.tile([P, 512], BF16, name="sc")
-        gexp = const.tile([P, NT * P], F32, name="gexp")
         gT = const.tile([P, NT * P], F32, name="gT")
-        Bsb = const.tile([P, 4096], BF16, name="Bsb")
-        Wsb = const.tile([P, 2048], BF16, name="Wsb")
-        Asb = const.tile([P, 1024], BF16, name="Asb")
+        Bsb = xin_pool.tile([P, 4096], BF16, name="Bsb", tag="xin7")
+        WAsb = const.tile([P, 3072], BF16, name="WAsb")
+        Wsb = WAsb[:, 0:2048]
+        Asb = WAsb[:, 2048:3072]
         Bq = const.tile([P, 1024], U32, name="Bq", align_bytes=64)
         Bs = const.tile([P, 1024], U8, name="Bs", align_bytes=64)
         Wq = const.tile([P, 512], U32, name="Wq", align_bytes=64)
         Ws = const.tile([P, 512], U8, name="Ws", align_bytes=64)
         Aq = const.tile([P, 256], U32, name="Aq", align_bytes=64)
         As = const.tile([P, 256], U8, name="As", align_bytes=64)
-        xin = [xin_pool.tile([P, 4096], BF16, name="xin%d" % i) for i in range(8)]
+        xin = {}
+        for i in range(7):
+            xin[i] = xin_pool.tile([P, 4096], BF16, name="xin%d" % i, tag="xin%d" % i)
 
         nc.vector.memset(warm[:], 0.0)
         nc.vector.memset(bbz[:], 0.0)
@@ -78,22 +87,24 @@ def tile_submatrixlinear_pa_t_kernel(tc, x, scores, Wb, bb, A, B, out):
             dst = xin[t0 // 4][:, (t0 % 4) * 1024 : (t0 % 4 + cnt) * 1024]
             nc.sync.dma_start(out=dst.rearrange("p (t i) -> p t i", i=1024), in_=x_v[:, t0 : t0 + cnt, :])
 
-        nc.sync.dma_start(out=sc[:].rearrange("p (t k) -> p t k", k=16), in_=scores.rearrange("(p t) k -> p t k", t=NT))
-        load_x(0, 2)
-        for j in range(4):
-            nc.sync.dma_start(out=Bsb[:, j * 1024 : (j + 1) * 1024], in_=B_v[:, j, :])
-        load_x(2, 2)
-        nc.sync.dma_start(out=Wsb[:].rearrange("p (h i) -> p h i", h=2), in_=Wb.rearrange("(h p) i -> p h i", p=P))
-        for h in range(2):
-            nc.sync.dma_start(
-                out=Asb[:, h * 512 : (h + 1) * 512].rearrange("p (k r) -> p k r", r=32),
-                in_=A[:, h * P : (h + 1) * P, :].rearrange("k p r -> p k r"),
-            )
-        nc.sync.dma_start(out=bbz[0:1, :], in_=bb.rearrange("(o n) -> o n", o=1))
-        load_x(4, 2)
-        load_x(6, 2)
-        for i in range(2, 8):
-            load_x(4 * i, 4)
+        for item in LOADS:
+            if item == "sc":
+                nc.sync.dma_start(out=sc[:].rearrange("p (t k) -> p t k", k=16), in_=scores.rearrange("(p t) k -> p t k", t=NT))
+            elif item == "B":
+                for j in range(4):
+                    nc.sync.dma_start(out=Bsb[:, j * 1024 : (j + 1) * 1024], in_=B_v[:, j, :])
+            elif item == "W":
+                nc.sync.dma_start(out=Wsb.rearrange("p (h i) -> p h i", h=2), in_=Wb.rearrange("(h p) i -> p h i", p=P))
+            elif item == "A":
+                for h in range(2):
+                    nc.sync.dma_start(
+                        out=Asb[:, h * 512 : (h + 1) * 512].rearrange("p (k r) -> p k r", r=32),
+                        in_=A[:, h * P : (h + 1) * P, :].rearrange("k p r -> p k r"),
+                    )
+            elif item == "bb":
+                nc.sync.dma_start(out=bbz[0:1, :], in_=bb.rearrange("(o n) -> o n", o=1))
+            else:
+                load_x(item[0], item[1])
 
         def t_rowtile(bk, src32, col0):
             for c in range(4):
@@ -101,6 +112,20 @@ def tile_submatrixlinear_pa_t_kernel(tc, x, scores, Wb, bb, A, B, out):
 
         def c_rowtile(bk, dst):
             nc.scalar.copy(out=dst, in_=bk[:].rearrange("p (g u n) -> p g n u", g=2, u=2))
+
+        gsrc4 = {}
+        gexps = {}
+
+        def emit_X(k):
+            t0, cnt = GROUPS[k]
+            ge = const.tile([P, cnt * P], F32, name="ge%d" % k)
+            gg, c0 = gsrc4[t0]
+            nc.gpsimd.tensor_scalar(
+                out=ge[:, 0 : cnt * P].rearrange("p (c r) -> p c r", r=8),
+                in0=gg[:, c0 : c0 + cnt * 16].unsqueeze(2).to_broadcast([P, cnt * 16, 8]),
+                scalar1=1.0, scalar2=0.0, op0=ALU.mult, op1=ALU.add,
+            )
+            gexps[k] = ge
 
         def gate_steps(part, ta, tb, on_pool):
             n = tb - ta
@@ -156,16 +181,9 @@ def tile_submatrixlinear_pa_t_kernel(tc, x, scores, Wb, bb, A, B, out):
             def st_g():
                 el.tensor_tensor(out=v3(gg), in0=v3(g1), in1=b3(r1), op=ALU.mult)
 
-            def st_expand(c0):
-                def f():
-                    nc.gpsimd.tensor_scalar(
-                        out=gexp[:, (ta + c0) * P : (ta + c0 + 4) * P].rearrange("p (c r) -> p c r", r=8),
-                        in0=gg[:, c0 * 16 : (c0 + 4) * 16].unsqueeze(2).to_broadcast([P, 64, 8]),
-                        scalar1=1.0, scalar2=0.0, op0=ALU.mult, op1=ALU.add,
-                    )
-                return f
-
-            return [st_max, st_sub, st_exp, st_sum, st_g0, st_thr, st_sum1, st_g] + [st_expand(c0) for c0 in range(0, n, 4)]
+            for t in range(ta, tb):
+                gsrc4[t] = (gg, (t - ta) * 16)
+            return [st_max, st_sub, st_exp, st_sum, st_g0, st_thr, st_sum1, st_g]
 
         xgs = {}
         xqs = {}
@@ -189,7 +207,7 @@ def tile_submatrixlinear_pa_t_kernel(tc, x, scores, Wb, bb, A, B, out):
             bk = bank("tp")
             for tt in range(cnt):
                 t = t0 + tt
-                nc.tensor.transpose(bk[:, tt * P : (tt + 1) * P], gexp[:, t * P : (t + 1) * P], ident[:])
+                nc.tensor.transpose(bk[:, tt * P : (tt + 1) * P], gexps[k][:, tt * P : (tt + 1) * P], ident[:])
             nc.scalar.copy(out=gT[:, t0 * P : (t0 + cnt) * P], in_=bk[:, 0 : cnt * P])
 
         def emit_Q(k):
@@ -241,7 +259,10 @@ def tile_submatrixlinear_pa_t_kernel(tc, x, scores, Wb, bb, A, B, out):
             xq, xs = xqs[k]
             hq, hs = hqs[k]
             if p0 == 0:
-                obs[k] = ob_pool.tile([P, 1024], F32, name="ob", tag="ob")
+                if cnt == 4:
+                    obs[k] = ob_pool.tile([P, 1024], F32, name="ob", tag="ob")
+                else:
+                    obs[k] = ob_pool.tile([P, 512], F32, name="obs", tag="obs")
             ob = obs[k]
             if True:
                 np_ = min(2, cnt - p0)
@@ -280,9 +301,11 @@ def tile_submatrixlinear_pa_t_kernel(tc, x, scores, Wb, bb, A, B, out):
         steps2[1]()
         for f in steps1[0:3]:
             f()
-        steps2[2]()
         for f in steps1[3:]:
             f()
+        for k in range(ng):
+            if GROUPS[k][0] < GATE_PARTS[0][1]:
+                emit_X(k)
         emit_T(0)
         Bg = xg_pool.tile([P, 4096], BF16, name="Bg", tag="xg", align_bytes=64)
         Bg32 = Bg[:].bitcast(F32)
@@ -291,6 +314,7 @@ def tile_submatrixlinear_pa_t_kernel(tc, x, scores, Wb, bb, A, B, out):
             bk = bank("tp")
             t_rowtile(bk, Bsb32, j * 512)
             c_rowtile(bk, Bg32[:, j * 512 : (j + 1) * 512].rearrange("p (g n u) -> p g n u", g=2, u=2))
+        steps2[2]()
         emit_Q(0)
         for hf in range(2):
             nc.vector.quantize_mx(
@@ -306,13 +330,13 @@ def tile_submatrixlinear_pa_t_kernel(tc, x, scores, Wb, bb, A, B, out):
         def prep_WA():
             WAg = xg_pool.tile([P, 4096], BF16, name="WAg", tag="xg", align_bytes=64)
             WAg32 = WAg[:].bitcast(F32)
-            Wsb32 = Wsb[:].bitcast(F32)
+            Wsb32 = Wsb.bitcast(F32)
             for h in range(2):
                 bk = bank("tp")
                 t_rowtile(bk, Wsb32, h * 512)
                 c_rowtile(bk, WAg32[:, 0:1024].rearrange("p (g h n u) -> p g h n u", g=2, h=2, u=2)[:, :, h])
             bk = bank("tp")
-            A4 = Asb[:].bitcast(F32).rearrange("p (h m u) -> p h m u", h=2, u=2)
+            A4 = Asb.bitcast(F32).rearrange("p (h m u) -> p h m u", h=2, u=2)
             for u in range(2):
                 for h in range(2):
                     nc.tensor.transpose(bk[:, u * 256 + h * P : u * 256 + (h + 1) * P], A4[:, h, :, u], ident[:])
@@ -333,26 +357,39 @@ def tile_submatrixlinear_pa_t_kernel(tc, x, scores, Wb, bb, A, B, out):
             nc.vector.quantize_mx(out=Aq[:].bitcast(FP8X4), scales=As[:], in_=WAg[:, 2048:3072])
 
         rest2 = steps2[6:]
-        for i in range(-1, ng):
-            if i + 2 < ng:
-                emit_T(i + 2)
-                emit_Tg(i + 2)
-            nu = GROUPS[i + 1][1] if i + 1 < ng else 0
-            no = GROUPS[i][1] if i >= 0 else 0
+        for i in range(1 - LT, ng + LO):
+            kt = i + LT
+            kg = i + LG
+            ko = i - LO
+            if kt == ng:
+                rot["u"] = [4, 5, 0, 1]
+                rot["o"] = [6, 7, 2, 3]
+            if kt < ng:
+                emit_T(kt)
+            if 1 <= kg < ng:
+                emit_Tg(kg)
+            if i == PREP_WA_AT:
+                wag = prep_WA()
+            nu = GROUPS[i][1] if 0 <= i < ng else 0
+            no = GROUPS[ko][1] if 0 <= ko < ng else 0
             for p0 in range(0, max(nu, no), 2):
                 if p0 < nu:
-                    emit_U(i + 1, p0)
+                    emit_U(i, p0)
                 if p0 < no:
-                    emit_O(i, p0)
-            if i + 2 < ng:
-                emit_Q(i + 2)
-            if i == -1:
-                for f in rest2[0:4]:
+                    emit_O(ko, p0)
+            if kt < ng:
+                emit_Q(kt)
+            if 0 <= i < ng:
+                emit_Hq(i)
+            if i == V3_AT:
+                for f in rest2:
                     f()
-            if i == 0:
-                for f in rest2[4:]:
-                    f()
-            if i + 1 < ng:
-                emit_Hq(i + 1)
-            if i == -1:
-                quant_WA(prep_WA())
+                for k in range(ng):
+                    if GROUPS[k][0] >= GATE_PARTS[0][1]:
+                        emit_X(k)
+            if i == PREP_WA_AT:
+                quant_WA(wag)
+            if i in LATE_LOADS:
+                d = LATE_LOADS[i]
+                xin[d] = xin_pool.tile([P, 4096], BF16, name="xin%d" % d, tag="xin%d" % d)
+                load_x(4 * d, 4)

@@ -18,14 +18,21 @@ FLOPS = 2 * 4096 * 1024 * 768 + 2 * 4096 * 512 * 256
 
 MANUAL = True
 GROUPS = [(0, 2), (2, 2), (4, 2), (6, 2), (8, 4), (12, 4), (16, 4), (20, 4), (24, 4), (28, 2), (30, 2)]
-E_ON_DVE_FROM = 7
+E_DVE = [7, 8, 9, 10]
+PREP_DVE = []
+CG_DVE = []
+CX_DVE = []
 GATE_PARTS = [(0, 8), (8, 32)]
 LT = 2
 LO = 3
 V3_AT = 0
-PREP_WA_AT = 2
+PREP = {2: ["W0", "W1", "A", "bias"]}
 LATE_LOADS = {2: 7}
 LOADS = ["sc", (0, 2), "B", (2, 2), (4, 2), (6, 2), "W", "bb", (8, 4), "A", (12, 4), (16, 4), (20, 4), (24, 4)]
+B_FIRST = False
+SPLIT_LAST = 0
+ROT = ([0, 1, 2, 3], [4, 5], [6, 7])
+ROUND_ROBIN = True
 LG = 1
 
 
@@ -44,10 +51,14 @@ def tile_submatrixlinear_pa_t_kernel(tc, x, scores, Wb, bb, A, B, out):
         if MANUAL:
             ctx.enter_context(tc.manual_schedule())
 
-        rot = {"tp": [0, 1, 2, 3], "u": [4, 5], "o": [6, 7]}
+        rot = {"tp": list(ROT[0]), "u": list(ROT[1]), "o": list(ROT[2])}
+        if ROUND_ROBIN:
+            rot["tp"] = [0, 1, 2, 3, 4, 5, 6, 7]
         cnt_rot = {"tp": 0, "u": 0, "o": 0}
 
         def bank(kind):
+            if ROUND_ROBIN:
+                kind = "tp"
             b = rot[kind][cnt_rot[kind] % len(rot[kind])]
             cnt_rot[kind] = cnt_rot[kind] + 1
             return psum.tile([P, 512], F32, name="bank%d" % b, tag="bank%d" % b)
@@ -110,8 +121,12 @@ def tile_submatrixlinear_pa_t_kernel(tc, x, scores, Wb, bb, A, B, out):
             for c in range(4):
                 nc.tensor.transpose(bk[:, c * P : (c + 1) * P], src32[:, col0 + c * P : col0 + (c + 1) * P], ident[:])
 
-        def c_rowtile(bk, dst):
-            nc.scalar.copy(out=dst, in_=bk[:].rearrange("p (g u n) -> p g n u", g=2, u=2))
+        def c_rowtile(bk, dst, on_vector=False):
+            src = bk[:].rearrange("p (g u n) -> p g n u", g=2, u=2)
+            if on_vector:
+                nc.vector.tensor_copy(out=dst, in_=src)
+            else:
+                nc.scalar.copy(out=dst, in_=src)
 
         gsrc4 = {}
         gexps = {}
@@ -199,7 +214,7 @@ def tile_submatrixlinear_pa_t_kernel(tc, x, scores, Wb, bb, A, B, out):
                 t = t0 + tt
                 bk = bank("tp")
                 t_rowtile(bk, xin[t // 4][:].bitcast(F32), (t % 4) * 512)
-                c_rowtile(bk, xg32[:, tt * 512 : (tt + 1) * 512].rearrange("p (g n u) -> p g n u", g=2, u=2))
+                c_rowtile(bk, xg32[:, tt * 512 : (tt + 1) * 512].rearrange("p (g n u) -> p g n u", g=2, u=2), on_vector=(k in CX_DVE and tt == cnt - 1))
             xgs[k] = xg
 
         def emit_Tg(k):
@@ -208,15 +223,18 @@ def tile_submatrixlinear_pa_t_kernel(tc, x, scores, Wb, bb, A, B, out):
             for tt in range(cnt):
                 t = t0 + tt
                 nc.tensor.transpose(bk[:, tt * P : (tt + 1) * P], gexps[k][:, tt * P : (tt + 1) * P], ident[:])
-            nc.scalar.copy(out=gT[:, t0 * P : (t0 + cnt) * P], in_=bk[:, 0 : cnt * P])
+            cp = nc.vector.tensor_copy if k in CG_DVE else nc.scalar.copy
+            cp(out=gT[:, t0 * P : (t0 + cnt) * P], in_=bk[:, 0 : cnt * P])
 
         def emit_Q(k):
             t0, cnt = GROUPS[k]
             xq = xq_pool.tile([P, 1024], U32, name="xq", tag="xq", align_bytes=64)
             xs = xq_pool.tile([P, 1024], U8, name="xs", tag="xs", align_bytes=64)
-            nc.vector.quantize_mx(
-                out=xq[:, 0 : cnt * 256].bitcast(FP8X4), scales=xs[:, 0 : cnt * 256], in_=xgs[k][:, 0 : cnt * 1024]
-            )
+            for a, n in ([(0, 2), (2, 1)] if cnt == 3 else [(0, cnt)]):
+                nc.vector.quantize_mx(
+                    out=xq[:, a * 256 : (a + n) * 256].bitcast(FP8X4), scales=xs[:, a * 256 : (a + n) * 256],
+                    in_=xgs[k][:, a * 1024 : (a + n) * 1024],
+                )
             xqs[k] = (xq, xs)
 
         def emit_U(k, p0):
@@ -249,23 +267,25 @@ def tile_submatrixlinear_pa_t_kernel(tc, x, scores, Wb, bb, A, B, out):
             t0, cnt = GROUPS[k]
             hq = hq_pool.tile([P, 512], U32, name="hq", tag="hq", align_bytes=64)
             hs = hq_pool.tile([P, 512], U8, name="hs", tag="hs", align_bytes=64)
-            nc.vector.quantize_mx(
-                out=hq[:, 0 : cnt * P].bitcast(FP8X4), scales=hs[:, 0 : cnt * P], in_=hgs[k][:, 0 : cnt * 512]
-            )
+            for a, n in ([(0, 2), (2, 1)] if cnt == 3 else [(0, cnt)]):
+                nc.vector.quantize_mx(
+                    out=hq[:, a * P : (a + n) * P].bitcast(FP8X4), scales=hs[:, a * P : (a + n) * P],
+                    in_=hgs[k][:, a * 512 : (a + n) * 512],
+                )
             hqs[k] = (hq, hs)
 
-        def emit_O(k, p0):
+        def emit_O(k, p0, wd=2):
             t0, cnt = GROUPS[k]
             xq, xs = xqs[k]
             hq, hs = hqs[k]
             if p0 == 0:
-                if cnt == 4:
+                if cnt >= 3:
                     obs[k] = ob_pool.tile([P, 1024], F32, name="ob", tag="ob")
                 else:
                     obs[k] = ob_pool.tile([P, 512], F32, name="obs", tag="obs")
             ob = obs[k]
             if True:
-                np_ = min(2, cnt - p0)
+                np_ = min(wd, cnt - p0)
                 bk = bank("o")
                 for q in range(np_):
                     tt = p0 + q
@@ -287,12 +307,14 @@ def tile_submatrixlinear_pa_t_kernel(tc, x, scores, Wb, bb, A, B, out):
                     )
                 w = np_ * 256
                 dst = ob[:, p0 * 256 : p0 * 256 + w]
-                if k >= E_ON_DVE_FROM:
+                if k in E_DVE:
                     nc.vector.tensor_tensor(out=dst, in0=bk[:, 0:w], in1=bb2[:, 0:w], op=ALU.add)
                 else:
                     nc.scalar.copy(out=dst, in_=bk[:, 0:w])
                     nc.gpsimd.tensor_tensor(out=dst, in0=dst, in1=bb2[:, 0:w], op=ALU.add)
-            if p0 + 2 >= cnt:
+            if wd == 1:
+                nc.sync.dma_start(out=out_v[:, t0 + p0, :], in_=ob[:, p0 * 256 : (p0 + 1) * 256])
+            elif p0 + 2 >= cnt:
                 nc.sync.dma_start(out=out_v[:, t0 : t0 + cnt, :], in_=ob[:, 0 : cnt * 256].rearrange("p (t o) -> p t o", o=256))
 
         steps1 = gate_steps(0, GATE_PARTS[0][0], GATE_PARTS[0][1], False)
@@ -306,7 +328,8 @@ def tile_submatrixlinear_pa_t_kernel(tc, x, scores, Wb, bb, A, B, out):
         for k in range(ng):
             if GROUPS[k][0] < GATE_PARTS[0][1]:
                 emit_X(k)
-        emit_T(0)
+        if not B_FIRST:
+            emit_T(0)
         Bg = xg_pool.tile([P, 4096], BF16, name="Bg", tag="xg", align_bytes=64)
         Bg32 = Bg[:].bitcast(F32)
         Bsb32 = Bsb[:].bitcast(F32)
@@ -314,47 +337,60 @@ def tile_submatrixlinear_pa_t_kernel(tc, x, scores, Wb, bb, A, B, out):
             bk = bank("tp")
             t_rowtile(bk, Bsb32, j * 512)
             c_rowtile(bk, Bg32[:, j * 512 : (j + 1) * 512].rearrange("p (g n u) -> p g n u", g=2, u=2))
-        steps2[2]()
-        emit_Q(0)
+        if B_FIRST:
+            emit_T(0)
+        else:
+            emit_Q(0)
         for hf in range(2):
             nc.vector.quantize_mx(
                 out=Bq[:, hf * 512 : (hf + 1) * 512].bitcast(FP8X4),
                 scales=Bs[:, hf * 512 : (hf + 1) * 512],
                 in_=Bg[:, hf * 2048 : (hf + 1) * 2048],
             )
+        if B_FIRST:
+            emit_Q(0)
+        steps2[2]()
         emit_Tg(0)
         steps2[3]()
         steps2[4]()
         steps2[5]()
 
-        def prep_WA():
-            WAg = xg_pool.tile([P, 4096], BF16, name="WAg", tag="xg", align_bytes=64)
-            WAg32 = WAg[:].bitcast(F32)
-            Wsb32 = Wsb.bitcast(F32)
-            for h in range(2):
-                bk = bank("tp")
-                t_rowtile(bk, Wsb32, h * 512)
-                c_rowtile(bk, WAg32[:, 0:1024].rearrange("p (g h n u) -> p g h n u", g=2, h=2, u=2)[:, :, h])
-            bk = bank("tp")
-            A4 = Asb.bitcast(F32).rearrange("p (h m u) -> p h m u", h=2, u=2)
-            for u in range(2):
-                for h in range(2):
-                    nc.tensor.transpose(bk[:, u * 256 + h * P : u * 256 + (h + 1) * P], A4[:, h, :, u], ident[:])
-            nc.scalar.copy(
-                out=WAg32[:, 1024:1536].rearrange("p (o u) -> p o u", u=2),
-                in_=bk[:].rearrange("p (u o) -> p o u", u=2),
-            )
-            bk = bank("tp")
-            nc.tensor.matmul(out=bk[:, 0:256], lhsT=ones[:], rhs=bbz[:], start=True, stop=True)
-            nc.scalar.copy(
-                out=bb2[:].rearrange("p (r o) -> p r o", r=2),
-                in_=bk[:, 0:256].unsqueeze(1).to_broadcast([P, 2, 256]),
-            )
-            return WAg
+        wag = {}
 
-        def quant_WA(WAg):
-            nc.vector.quantize_mx(out=Wq[:].bitcast(FP8X4), scales=Ws[:], in_=WAg[:, 0:2048])
-            nc.vector.quantize_mx(out=Aq[:].bitcast(FP8X4), scales=As[:], in_=WAg[:, 2048:3072])
+        def prep_piece(what):
+            if "t" not in wag:
+                wag["t"] = xg_pool.tile([P, 3072], BF16, name="WAg", tag="wag", bufs=1, align_bytes=64)
+            WAg = wag["t"]
+            WAg32 = WAg[:].bitcast(F32)
+            bk = bank("tp")
+            if what == "W0" or what == "W1":
+                h = 0 if what == "W0" else 1
+                t_rowtile(bk, Wsb.bitcast(F32), h * 512)
+                c_rowtile(bk, WAg32[:, 0:1024].rearrange("p (g h n u) -> p g h n u", g=2, h=2, u=2)[:, :, h], on_vector=(what in PREP_DVE))
+            elif what == "A":
+                A4 = Asb.bitcast(F32).rearrange("p (h m u) -> p h m u", h=2, u=2)
+                for u in range(2):
+                    for h in range(2):
+                        nc.tensor.transpose(bk[:, u * 256 + h * P : u * 256 + (h + 1) * P], A4[:, h, :, u], ident[:])
+                cp = nc.vector.tensor_copy if what in PREP_DVE else nc.scalar.copy
+                cp(
+                    out=WAg32[:, 1024:1536].rearrange("p (o u) -> p o u", u=2),
+                    in_=bk[:].rearrange("p (u o) -> p o u", u=2),
+                )
+            else:
+                nc.tensor.matmul(out=bk[:, 0:256], lhsT=ones[:], rhs=bbz[:], start=True, stop=True)
+                cp = nc.vector.tensor_copy if what in PREP_DVE else nc.scalar.copy
+                cp(
+                    out=bb2[:].rearrange("p (r o) -> p r o", r=2),
+                    in_=bk[:, 0:256].unsqueeze(1).to_broadcast([P, 2, 256]),
+                )
+
+        def quant_piece(what):
+            WAg = wag["t"]
+            if what == "W1":
+                nc.vector.quantize_mx(out=Wq[:].bitcast(FP8X4), scales=Ws[:], in_=WAg[:, 0:2048])
+            if what == "A":
+                nc.vector.quantize_mx(out=Aq[:].bitcast(FP8X4), scales=As[:], in_=WAg[:, 2048:3072])
 
         rest2 = steps2[6:]
         for i in range(1 - LT, ng + LO):
@@ -362,21 +398,25 @@ def tile_submatrixlinear_pa_t_kernel(tc, x, scores, Wb, bb, A, B, out):
             kg = i + LG
             ko = i - LO
             if kt == ng:
-                rot["u"] = [4, 5, 0, 1]
-                rot["o"] = [6, 7, 2, 3]
+                rot["u"] = list(ROT[1]) + list(ROT[0][0:2])
+                rot["o"] = list(ROT[2]) + list(ROT[0][2:])
             if kt < ng:
                 emit_T(kt)
             if 1 <= kg < ng:
                 emit_Tg(kg)
-            if i == PREP_WA_AT:
-                wag = prep_WA()
+            for what in PREP.get(i, []):
+                prep_piece(what)
             nu = GROUPS[i][1] if 0 <= i < ng else 0
             no = GROUPS[ko][1] if 0 <= ko < ng else 0
             for p0 in range(0, max(nu, no), 2):
                 if p0 < nu:
                     emit_U(i, p0)
                 if p0 < no:
-                    emit_O(ko, p0)
+                    if ko >= ng - SPLIT_LAST:
+                        emit_O(ko, p0, 1)
+                        emit_O(ko, p0 + 1, 1)
+                    else:
+                        emit_O(ko, p0)
             if kt < ng:
                 emit_Q(kt)
             if 0 <= i < ng:
@@ -387,8 +427,8 @@ def tile_submatrixlinear_pa_t_kernel(tc, x, scores, Wb, bb, A, B, out):
                 for k in range(ng):
                     if GROUPS[k][0] >= GATE_PARTS[0][1]:
                         emit_X(k)
-            if i == PREP_WA_AT:
-                quant_WA(wag)
+            for what in PREP.get(i, []):
+                quant_piece(what)
             if i in LATE_LOADS:
                 d = LATE_LOADS[i]
                 xin[d] = xin_pool.tile([P, 4096], BF16, name="xin%d" % d, tag="xin%d" % d)

@@ -18,17 +18,17 @@ FLOPS = 2 * 4096 * 1024 * 768 + 2 * 4096 * 512 * 256
 
 MANUAL = True
 GROUPS = [(0, 2), (2, 2), (4, 2), (6, 2), (8, 4), (12, 4), (16, 4), (20, 4), (24, 4), (28, 2), (30, 2)]
-E_DVE = [7, 8, 9, 10]
+E_DVE = [0, 1, 2, 3, 4, 5, 6, 7, 8, 9, 10]
 PREP_DVE = []
 CG_DVE = []
 CX_DVE = []
 GATE_PARTS = [(0, 8), (8, 32)]
 LT = 2
-LO = 3
+LO = 4
 V3_AT = 0
-PREP = {2: ["W0", "W1", "A", "bias"]}
+PREP = {1: ["W0"], 2: ["W1", "bias"], 3: ["A"]}
 LATE_LOADS = {2: 7}
-LOADS = ["sc", (0, 2), "B", (2, 2), (4, 2), (6, 2), "W", "bb", (8, 4), "A", (12, 4), (16, 4), (20, 4), (24, 4)]
+LOADS = ["sc", (0, 2), "B", (2, 2), (4, 2), (6, 2), "W", "bb", (8, 4), (12, 4), "A", (16, 4), (20, 4), (24, 4)]
 B_FIRST = False
 SPLIT_LAST = 0
 ROT = ([0, 1, 2, 3], [4, 5], [6, 7])

@@ -181,12 +181,7 @@ def tile_submatrixlinear_pa_t_kernel(tc, x, scores, Wb, bb, A, B, out):
                 el.tensor_tensor(out=v3(g0), in0=v3(ee), in1=b3(rs), op=ALU.mult)
 
             def st_thr():
-                if on_pool:
-                    mk = const.tile([P, w], F32, name="mk%d" % part)
-                    nc.gpsimd.tensor_scalar(out=mk[:], in0=g0[:], scalar1=0.05, scalar2=1.0, op0=ALU.is_gt, op1=ALU.mult)
-                    nc.gpsimd.tensor_tensor(out=g1[:], in0=mk[:], in1=g0[:], op=ALU.mult)
-                else:
-                    nc.vector.scalar_tensor_tensor(out=g1[:], in0=g0[:], scalar=0.05, in1=g0[:], op0=ALU.is_gt, op1=ALU.mult)
+                nc.vector.scalar_tensor_tensor(out=g1[:], in0=g0[:], scalar=0.05, in1=g0[:], op0=ALU.is_gt, op1=ALU.mult)
 
             def st_sum1():
                 nc.vector.tensor_reduce(out=s1[:], in_=v3(g1), axis=AX.X, op=ALU.add)
@@ -350,10 +345,8 @@ def tile_submatrixlinear_pa_t_kernel(tc, x, scores, Wb, bb, A, B, out):
         if B_FIRST:
             emit_Q(0)
         steps2[2]()
-        emit_Tg(0)
         steps2[3]()
         steps2[4]()
-        steps2[5]()
 
         wag = {}
 
@@ -392,7 +385,7 @@ def tile_submatrixlinear_pa_t_kernel(tc, x, scores, Wb, bb, A, B, out):
             if what == "A":
                 nc.vector.quantize_mx(out=Aq[:].bitcast(FP8X4), scales=As[:], in_=WAg[:, 2048:3072])
 
-        rest2 = steps2[6:]
+        rest2 = steps2[5:]
         for i in range(1 - LT, ng + LO):
             kt = i + LT
             kg = i + LG
@@ -402,7 +395,7 @@ def tile_submatrixlinear_pa_t_kernel(tc, x, scores, Wb, bb, A, B, out):
                 rot["o"] = list(ROT[2]) + list(ROT[0][2:])
             if kt < ng:
                 emit_T(kt)
-            if 1 <= kg < ng:
+            if 0 <= kg < ng:
                 emit_Tg(kg)
             for what in PREP.get(i, []):
                 prep_piece(what)

@@ -25,10 +25,11 @@ CX_DVE = []
 GATE_PARTS = [(0, 8), (8, 32)]
 LT = 2
 LO = 4
-V3_AT = 0
+TRIP_AT = 1
+ON_POOL = []
 PREP = {1: ["W0"], 2: ["W1", "bias"], 3: ["A"]}
 LATE_LOADS = {2: 7}
-LOADS = ["sc", (0, 2), "B", (2, 2), (4, 2), (6, 2), "W", "bb", (8, 4), (12, 4), "A", (16, 4), (20, 4), (24, 4)]
+LOADS = ["sc", (0, 2), "B", (2, 2), (4, 2), (6, 2), "W", "bb", (8, 4), (12, 4), "A", (16, 4)]
 B_FIRST = False
 SPLIT_LAST = 0
 ROT = ([0, 1, 2, 3], [4, 5], [6, 7])
@@ -69,7 +70,9 @@ def tile_submatrixlinear_pa_t_kernel(tc, x, scores, Wb, bb, A, B, out):
         bb2 = const.tile([P, 512], F32, name="bb2")
         warm = const.tile([P, 1], F32, name="warm")
         sc = const.tile([P, 512], BF16, name="sc")
-        gT = const.tile([P, NT * P], F32, name="gT")
+        gT = const.tile([P, 8 * P], F32, name="gT")
+        gT2 = const.tile([P, 24 * P], F32, name="gT2")
+        gc = const.tile([P, 3 * P], F32, name="gc")
         Bsb = xin_pool.tile([P, 4096], BF16, name="Bsb", tag="xin7")
         WAsb = const.tile([P, 3072], BF16, name="WAsb")
         Wsb = WAsb[:, 0:2048]
@@ -150,13 +153,14 @@ def tile_submatrixlinear_pa_t_kernel(tc, x, scores, Wb, bb, A, B, out):
             dd = const.tile([P, w], F32, name="dd%d" % part)
             ee = const.tile([P, w], F32, name="ee%d" % part)
             ss = const.tile([P, n], F32, name="ss%d" % part)
-            rs = const.tile([P, n], F32, name="rs%d" % part)
             g0 = const.tile([P, w], F32, name="g0%d" % part)
             g1 = const.tile([P, w], F32, name="g1%d" % part)
             s1 = const.tile([P, n], F32, name="s1%d" % part)
             r1 = const.tile([P, n], F32, name="r1%d" % part)
             gg = const.tile([P, w], F32, name="gg%d" % part)
-            el = nc.gpsimd if on_pool else nc.vector
+            el_sub = nc.gpsimd if "sub" in on_pool else nc.vector
+            el_thr = nc.gpsimd if "thr" in on_pool else nc.vector
+            el_g = nc.gpsimd if "g" in on_pool else nc.vector
 
             def v3(t):
                 return t[:].rearrange("p (t k) -> p t k", k=16)
@@ -168,28 +172,26 @@ def tile_submatrixlinear_pa_t_kernel(tc, x, scores, Wb, bb, A, B, out):
                 nc.vector.tensor_reduce(out=mx[:], in_=s3, axis=AX.X, op=ALU.max)
 
             def st_sub():
-                el.tensor_tensor(out=v3(dd), in0=s3, in1=b3(mx), op=ALU.subtract)
+                el_sub.tensor_tensor(out=v3(dd), in0=s3, in1=b3(mx), op=ALU.subtract)
 
             def st_exp():
                 nc.scalar.activation(out=ee[:], in_=dd[:], func=ACT.Exp)
 
             def st_sum():
                 nc.vector.tensor_reduce(out=ss[:], in_=v3(ee), axis=AX.X, op=ALU.add)
-                nc.vector.reciprocal(out=rs[:], in_=ss[:])
 
             def st_g0():
-                el.tensor_tensor(out=v3(g0), in0=v3(ee), in1=b3(rs), op=ALU.mult)
+                nc.vector.scalar_tensor_tensor(out=v3(g0), in0=v3(ee), scalar=20.0, in1=b3(ss), op0=ALU.mult, op1=ALU.is_gt)
 
             def st_thr():
-                nc.vector.scalar_tensor_tensor(out=g1[:], in0=g0[:], scalar=0.05, in1=g0[:], op0=ALU.is_gt, op1=ALU.mult)
+                el_thr.tensor_tensor(out=g1[:], in0=g0[:], in1=ee[:], op=ALU.mult)
 
             def st_sum1():
                 nc.vector.tensor_reduce(out=s1[:], in_=v3(g1), axis=AX.X, op=ALU.add)
-                nc.vector.tensor_scalar_max(out=s1[:], in0=s1[:], scalar1=1e-8)
                 nc.vector.reciprocal(out=r1[:], in_=s1[:])
 
             def st_g():
-                el.tensor_tensor(out=v3(gg), in0=v3(g1), in1=b3(r1), op=ALU.mult)
+                el_g.tensor_tensor(out=v3(gg), in0=v3(g1), in1=b3(r1), op=ALU.mult)
 
             for t in range(ta, tb):
                 gsrc4[t] = (gg, (t - ta) * 16)
@@ -221,6 +223,20 @@ def tile_submatrixlinear_pa_t_kernel(tc, x, scores, Wb, bb, A, B, out):
             cp = nc.vector.tensor_copy if k in CG_DVE else nc.scalar.copy
             cp(out=gT[:, t0 * P : (t0 + cnt) * P], in_=bk[:, 0 : cnt * P])
 
+        def emit_trip():
+            gg, c0 = gsrc4[8]
+            bk = bank("tp")
+            for c in range(3):
+                nc.tensor.transpose(bk[:, c * P : (c + 1) * P], gg[:, c * P : (c + 1) * P], ident[:])
+            nc.scalar.copy(out=gc[:], in_=bk[:, 0 : 3 * P])
+            scratch = out[0:192, :].rearrange("n o -> (n o)").rearrange("(p c) -> p c", c=384)
+            nc.sync.dma_start(out=scratch, in_=gc[:])
+            src = scratch.rearrange("(t k) n -> k t n", k=16)
+            for r in range(8):
+                nc.sync.dma_start(out=gT2[r:P:8, :].rearrange("p (t n) -> p t n", n=384), in_=src)
+            load_x(20, 4)
+            load_x(24, 4)
+
         def emit_Q(k):
             t0, cnt = GROUPS[k]
             xq = xq_pool.tile([P, 1024], U32, name="xq", tag="xq", align_bytes=64)
@@ -231,6 +247,12 @@ def tile_submatrixlinear_pa_t_kernel(tc, x, scores, Wb, bb, A, B, out):
                     in_=xgs[k][:, a * 1024 : (a + n) * 1024],
                 )
             xqs[k] = (xq, xs)
+
+        def gate_block(t):
+            if t < 8:
+                return gT[:, t * P : (t + 1) * P]
+            b = 3 * ((t - 8) % 8) + (t - 8) // 8
+            return gT2[:, b * P : (b + 1) * P]
 
         def emit_U(k, p0):
             t0, cnt = GROUPS[k]
@@ -254,7 +276,7 @@ def tile_submatrixlinear_pa_t_kernel(tc, x, scores, Wb, bb, A, B, out):
                 nc.vector.tensor_tensor(
                     out=hg[:, tt * 512 : (tt + 1) * 512].rearrange("p (n j) -> p n j", j=4),
                     in0=bk[:].rearrange("p (j n) -> p n j", j=4),
-                    in1=gT[:, t * P : (t + 1) * P].unsqueeze(2).to_broadcast([P, P, 4]),
+                    in1=gate_block(t).unsqueeze(2).to_broadcast([P, P, 4]),
                     op=ALU.mult,
                 )
 
@@ -312,13 +334,15 @@ def tile_submatrixlinear_pa_t_kernel(tc, x, scores, Wb, bb, A, B, out):
             elif p0 + 2 >= cnt:
                 nc.sync.dma_start(out=out_v[:, t0 : t0 + cnt, :], in_=ob[:, 0 : cnt * 256].rearrange("p (t o) -> p t o", o=256))
 
-        steps1 = gate_steps(0, GATE_PARTS[0][0], GATE_PARTS[0][1], False)
-        steps2 = gate_steps(1, GATE_PARTS[1][0], GATE_PARTS[1][1], True)
-        steps2[0]()
-        steps2[1]()
+        steps1 = gate_steps(0, GATE_PARTS[0][0], GATE_PARTS[0][1], [])
+        steps2 = gate_steps(1, GATE_PARTS[1][0], GATE_PARTS[1][1], ON_POOL)
         for f in steps1[0:3]:
             f()
+        for f in steps2[0:3]:
+            f()
         for f in steps1[3:]:
+            f()
+        for f in steps2[3:5]:
             f()
         for k in range(ng):
             if GROUPS[k][0] < GATE_PARTS[0][1]:
@@ -344,9 +368,8 @@ def tile_submatrixlinear_pa_t_kernel(tc, x, scores, Wb, bb, A, B, out):
             )
         if B_FIRST:
             emit_Q(0)
-        steps2[2]()
-        steps2[3]()
-        steps2[4]()
+        for f in steps2[5:]:
+            f()
 
         wag = {}
 
@@ -385,7 +408,6 @@ def tile_submatrixlinear_pa_t_kernel(tc, x, scores, Wb, bb, A, B, out):
             if what == "A":
                 nc.vector.quantize_mx(out=Aq[:].bitcast(FP8X4), scales=As[:], in_=WAg[:, 2048:3072])
 
-        rest2 = steps2[5:]
         for i in range(1 - LT, ng + LO):
             kt = i + LT
             kg = i + LG
@@ -395,8 +417,10 @@ def tile_submatrixlinear_pa_t_kernel(tc, x, scores, Wb, bb, A, B, out):
                 rot["o"] = list(ROT[2]) + list(ROT[0][2:])
             if kt < ng:
                 emit_T(kt)
-            if 0 <= kg < ng:
+            if 0 <= kg < ng and GROUPS[kg][0] < GATE_PARTS[0][1]:
                 emit_Tg(kg)
+            if i == TRIP_AT:
+                emit_trip()
             for what in PREP.get(i, []):
                 prep_piece(what)
             nu = GROUPS[i][1] if 0 <= i < ng else 0
@@ -414,12 +438,6 @@ def tile_submatrixlinear_pa_t_kernel(tc, x, scores, Wb, bb, A, B, out):
                 emit_Q(kt)
             if 0 <= i < ng:
                 emit_Hq(i)
-            if i == V3_AT:
-                for f in rest2:
-                    f()
-                for k in range(ng):
-                    if GROUPS[k][0] >= GATE_PARTS[0][1]:
-                        emit_X(k)
             for what in PREP.get(i, []):
                 quant_piece(what)
             if i in LATE_LOADS:

@@ -22,14 +22,15 @@ E_DVE = [0, 1, 2, 3, 4, 5, 6, 7, 8, 9, 10]
 PREP_DVE = []
 CG_DVE = []
 CX_DVE = []
-GATE_PARTS = [(0, 8), (8, 32)]
+GATE_PARTS = [(0, 16), (16, 32)]
 LT = 2
 LO = 4
-TRIP_AT = 1
+TRIP_AT = 3
+GATES2 = {-1: (0, 2), 0: (2, 4), 1: (4, 8)}
 ON_POOL = []
 PREP = {1: ["W0"], 2: ["W1", "bias"], 3: ["A"]}
 LATE_LOADS = {2: 7}
-LOADS = ["sc", (0, 2), "B", (2, 2), (4, 2), (6, 2), "W", "bb", (8, 4), (12, 4), "A", (16, 4)]
+LOADS = ["sc", (0, 2), "B", (2, 2), (4, 2), (6, 2), "W", "bb", (8, 4), (12, 4), "A", (16, 4), (20, 4), (24, 4)]
 B_FIRST = False
 SPLIT_LAST = 0
 ROT = ([0, 1, 2, 3], [4, 5], [6, 7])
@@ -70,9 +71,9 @@ def tile_submatrixlinear_pa_t_kernel(tc, x, scores, Wb, bb, A, B, out):
         bb2 = const.tile([P, 512], F32, name="bb2")
         warm = const.tile([P, 1], F32, name="warm")
         sc = const.tile([P, 512], BF16, name="sc")
-        gT = const.tile([P, 8 * P], F32, name="gT")
-        gT2 = const.tile([P, 24 * P], F32, name="gT2")
-        gc = const.tile([P, 3 * P], F32, name="gc")
+        gT = const.tile([P, 16 * P], F32, name="gT")
+        gT2 = const.tile([P, 16 * P], F32, name="gT2")
+        gc = const.tile([P, 2 * P], F32, name="gc")
         Bsb = xin_pool.tile([P, 4096], BF16, name="Bsb", tag="xin7")
         WAsb = const.tile([P, 3072], BF16, name="WAsb")
         Wsb = WAsb[:, 0:2048]
@@ -224,18 +225,16 @@ def tile_submatrixlinear_pa_t_kernel(tc, x, scores, Wb, bb, A, B, out):
             cp(out=gT[:, t0 * P : (t0 + cnt) * P], in_=bk[:, 0 : cnt * P])
 
         def emit_trip():
-            gg, c0 = gsrc4[8]
+            gg, c0 = gsrc4[16]
             bk = bank("tp")
-            for c in range(3):
+            for c in range(2):
                 nc.tensor.transpose(bk[:, c * P : (c + 1) * P], gg[:, c * P : (c + 1) * P], ident[:])
-            nc.scalar.copy(out=gc[:], in_=bk[:, 0 : 3 * P])
-            scratch = out[0:192, :].rearrange("n o -> (n o)").rearrange("(p c) -> p c", c=384)
+            nc.scalar.copy(out=gc[:], in_=bk[:, 0 : 2 * P])
+            scratch = out[0:P, :]
             nc.sync.dma_start(out=scratch, in_=gc[:])
             src = scratch.rearrange("(t k) n -> k t n", k=16)
             for r in range(8):
-                nc.sync.dma_start(out=gT2[r:P:8, :].rearrange("p (t n) -> p t n", n=384), in_=src)
-            load_x(20, 4)
-            load_x(24, 4)
+                nc.sync.dma_start(out=gT2[r:P:8, :].rearrange("p (t n) -> p t n", n=256), in_=src)
 
         def emit_Q(k):
             t0, cnt = GROUPS[k]
@@ -249,9 +248,9 @@ def tile_submatrixlinear_pa_t_kernel(tc, x, scores, Wb, bb, A, B, out):
             xqs[k] = (xq, xs)
 
         def gate_block(t):
-            if t < 8:
+            if t < 16:
                 return gT[:, t * P : (t + 1) * P]
-            b = 3 * ((t - 8) % 8) + (t - 8) // 8
+            b = 2 * ((t - 16) % 8) + (t - 16) // 8
             return gT2[:, b * P : (b + 1) * P]
 
         def emit_U(k, p0):
@@ -338,11 +337,7 @@ def tile_submatrixlinear_pa_t_kernel(tc, x, scores, Wb, bb, A, B, out):
         steps2 = gate_steps(1, GATE_PARTS[1][0], GATE_PARTS[1][1], ON_POOL)
         for f in steps1[0:3]:
             f()
-        for f in steps2[0:3]:
-            f()
         for f in steps1[3:]:
-            f()
-        for f in steps2[3:5]:
             f()
         for k in range(ng):
             if GROUPS[k][0] < GATE_PARTS[0][1]:
@@ -368,8 +363,6 @@ def tile_submatrixlinear_pa_t_kernel(tc, x, scores, Wb, bb, A, B, out):
             )
         if B_FIRST:
             emit_Q(0)
-        for f in steps2[5:]:
-            f()
 
         wag = {}
 
@@ -438,6 +431,9 @@ def tile_submatrixlinear_pa_t_kernel(tc, x, scores, Wb, bb, A, B, out):
                 emit_Q(kt)
             if 0 <= i < ng:
                 emit_Hq(i)
+            if i in GATES2:
+                for f in steps2[GATES2[i][0] : GATES2[i][1]]:
+                    f()
             for what in PREP.get(i, []):
                 quant_piece(what)
             if i in LATE_LOADS:

@@ -78,12 +78,12 @@ def tile_submatrixlinear_pa_t_kernel(tc, x, scores, Wb, bb, A, B, out):
         WAsb = const.tile([P, 3072], BF16, name="WAsb")
         Wsb = WAsb[:, 0:2048]
         Asb = WAsb[:, 2048:3072]
-        Bq = const.tile([P, 1024], U32, name="Bq", align_bytes=64)
-        Bs = const.tile([P, 1024], U8, name="Bs", align_bytes=64)
-        Wq = const.tile([P, 512], U32, name="Wq", align_bytes=64)
-        Ws = const.tile([P, 512], U8, name="Ws", align_bytes=64)
-        Aq = const.tile([P, 256], U32, name="Aq", align_bytes=64)
-        As = const.tile([P, 256], U8, name="As", align_bytes=64)
+        Bq = const.tile([P, 1024], U32, name="Bq", align_bytes=256)
+        Bs = const.tile([P, 1024], U8, name="Bs", align_bytes=256)
+        Wq = const.tile([P, 512], U32, name="Wq", align_bytes=256)
+        Ws = const.tile([P, 512], U8, name="Ws", align_bytes=256)
+        Aq = const.tile([P, 256], U32, name="Aq", align_bytes=256)
+        As = const.tile([P, 256], U8, name="As", align_bytes=256)
         xin = {}
         for i in range(7):
             xin[i] = xin_pool.tile([P, 4096], BF16, name="xin%d" % i, tag="xin%d" % i)
@@ -206,7 +206,7 @@ def tile_submatrixlinear_pa_t_kernel(tc, x, scores, Wb, bb, A, B, out):
 
         def emit_T(k):
             t0, cnt = GROUPS[k]
-            xg = xg_pool.tile([P, 4096], BF16, name="xg", tag="xg", align_bytes=64)
+            xg = xg_pool.tile([P, 4096], BF16, name="xg", tag="xg", align_bytes=256)
             xg32 = xg[:].bitcast(F32)
             for tt in range(cnt):
                 t = t0 + tt
@@ -238,8 +238,8 @@ def tile_submatrixlinear_pa_t_kernel(tc, x, scores, Wb, bb, A, B, out):
 
         def emit_Q(k):
             t0, cnt = GROUPS[k]
-            xq = xq_pool.tile([P, 1024], U32, name="xq", tag="xq", align_bytes=64)
-            xs = xq_pool.tile([P, 1024], U8, name="xs", tag="xs", align_bytes=64)
+            xq = xq_pool.tile([P, 1024], U32, name="xq", tag="xq", align_bytes=256)
+            xs = xq_pool.tile([P, 1024], U8, name="xs", tag="xs", align_bytes=256)
             for a, n in ([(0, 2), (2, 1)] if cnt == 3 else [(0, cnt)]):
                 nc.vector.quantize_mx(
                     out=xq[:, a * 256 : (a + n) * 256].bitcast(FP8X4), scales=xs[:, a * 256 : (a + n) * 256],
@@ -257,7 +257,7 @@ def tile_submatrixlinear_pa_t_kernel(tc, x, scores, Wb, bb, A, B, out):
             t0, cnt = GROUPS[k]
             xq, xs = xqs[k]
             if p0 == 0:
-                hgs[k] = h_pool.tile([P, 2048], BF16, name="hg", tag="hg", align_bytes=64)
+                hgs[k] = h_pool.tile([P, 2048], BF16, name="hg", tag="hg", align_bytes=256)
             hg = hgs[k]
             for tt in range(p0, min(p0 + 2, cnt)):
                 t = t0 + tt
@@ -281,8 +281,8 @@ def tile_submatrixlinear_pa_t_kernel(tc, x, scores, Wb, bb, A, B, out):
 
         def emit_Hq(k):
             t0, cnt = GROUPS[k]
-            hq = hq_pool.tile([P, 512], U32, name="hq", tag="hq", align_bytes=64)
-            hs = hq_pool.tile([P, 512], U8, name="hs", tag="hs", align_bytes=64)
+            hq = hq_pool.tile([P, 512], U32, name="hq", tag="hq", align_bytes=256)
+            hs = hq_pool.tile([P, 512], U8, name="hs", tag="hs", align_bytes=256)
             for a, n in ([(0, 2), (2, 1)] if cnt == 3 else [(0, cnt)]):
                 nc.vector.quantize_mx(
                     out=hq[:, a * P : (a + n) * P].bitcast(FP8X4), scales=hs[:, a * P : (a + n) * P],
@@ -344,7 +344,7 @@ def tile_submatrixlinear_pa_t_kernel(tc, x, scores, Wb, bb, A, B, out):
                 emit_X(k)
         if not B_FIRST:
             emit_T(0)
-        Bg = xg_pool.tile([P, 4096], BF16, name="Bg", tag="xg", align_bytes=64)
+        Bg = xg_pool.tile([P, 4096], BF16, name="Bg", tag="xg", align_bytes=256)
         Bg32 = Bg[:].bitcast(F32)
         Bsb32 = Bsb[:].bitcast(F32)
         for j in range(4):
@@ -368,7 +368,7 @@ def tile_submatrixlinear_pa_t_kernel(tc, x, scores, Wb, bb, A, B, out):
 
         def prep_piece(what):
             if "t" not in wag:
-                wag["t"] = xg_pool.tile([P, 3072], BF16, name="WAg", tag="wag", bufs=1, align_bytes=64)
+                wag["t"] = xg_pool.tile([P, 3072], BF16, name="WAg", tag="wag", bufs=1, align_bytes=256)
             WAg = wag["t"]
             WAg32 = WAg[:].bitcast(F32)
             bk = bank("tp")

@@ -22,11 +22,12 @@ E_DVE = [0, 1, 2, 3, 4, 5, 6, 7, 8, 9, 10]
 PREP_DVE = []
 CG_DVE = []
 CX_DVE = []
-GATE_PARTS = [(0, 16), (16, 32)]
+GATE_PARTS = [(0, 8), (8, 16), (16, 24), (24, 32)]
 LT = 2
 LO = 4
 TRIP_AT = 3
-GATES2 = {-1: (0, 2), 0: (2, 4), 1: (4, 8)}
+LATE_MID = {0: (3, 5), 1: (6, 7)}
+LATE_END = {-1: (2, 3), 0: (5, 6), 1: (7, 9)}
 ON_POOL = []
 PREP = {1: ["W0"], 2: ["W1", "bias"], 3: ["A"]}
 LATE_LOADS = {2: 7}
@@ -73,6 +74,7 @@ def tile_submatrixlinear_pa_t_kernel(tc, x, scores, Wb, bb, A, B, out):
         sc = const.tile([P, 512], BF16, name="sc")
         gT = const.tile([P, 16 * P], F32, name="gT")
         gT2 = const.tile([P, 16 * P], F32, name="gT2")
+        Ar = const.tile([P, 512], F32, name="Ar")
         gc = const.tile([P, 2 * P], F32, name="gc")
         Bsb = xin_pool.tile([P, 4096], BF16, name="Bsb", tag="xin7")
         WAsb = const.tile([P, 3072], BF16, name="WAsb")
@@ -111,11 +113,9 @@ def tile_submatrixlinear_pa_t_kernel(tc, x, scores, Wb, bb, A, B, out):
             elif item == "W":
                 nc.sync.dma_start(out=Wsb.rearrange("p (h i) -> p h i", h=2), in_=Wb.rearrange("(h p) i -> p h i", p=P))
             elif item == "A":
-                for h in range(2):
-                    nc.sync.dma_start(
-                        out=Asb[:, h * 512 : (h + 1) * 512].rearrange("p (k r) -> p k r", r=32),
-                        in_=A[:, h * P : (h + 1) * P, :].rearrange("k p r -> p k r"),
-                    )
+                nc.sync.dma_start(
+                    out=Asb.rearrange("p (k c) -> p k c", c=64), in_=A.rearrange("k (p h) r -> p k (h r)", h=2)
+                )
             elif item == "bb":
                 nc.sync.dma_start(out=bbz[0:1, :], in_=bb.rearrange("(o n) -> o n", o=1))
             else:
@@ -189,6 +189,8 @@ def tile_submatrixlinear_pa_t_kernel(tc, x, scores, Wb, bb, A, B, out):
 
             def st_sum1():
                 nc.vector.tensor_reduce(out=s1[:], in_=v3(g1), axis=AX.X, op=ALU.add)
+
+            def st_rec():
                 nc.vector.reciprocal(out=r1[:], in_=s1[:])
 
             def st_g():
@@ -196,7 +198,7 @@ def tile_submatrixlinear_pa_t_kernel(tc, x, scores, Wb, bb, A, B, out):
 
             for t in range(ta, tb):
                 gsrc4[t] = (gg, (t - ta) * 16)
-            return [st_max, st_sub, st_exp, st_sum, st_g0, st_thr, st_sum1, st_g]
+            return [st_max, st_sub, st_exp, st_sum, st_g0, st_thr, st_sum1, st_rec, st_g]
 
         xgs = {}
         xqs = {}
@@ -225,10 +227,9 @@ def tile_submatrixlinear_pa_t_kernel(tc, x, scores, Wb, bb, A, B, out):
             cp(out=gT[:, t0 * P : (t0 + cnt) * P], in_=bk[:, 0 : cnt * P])
 
         def emit_trip():
-            gg, c0 = gsrc4[16]
             bk = bank("tp")
             for c in range(2):
-                nc.tensor.transpose(bk[:, c * P : (c + 1) * P], gg[:, c * P : (c + 1) * P], ident[:])
+                nc.tensor.transpose(bk[:, c * P : (c + 1) * P], gsrc4[16 + 8 * c][0][:], ident[:])
             nc.scalar.copy(out=gc[:], in_=bk[:, 0 : 2 * P])
             scratch = out[0:P, :]
             nc.sync.dma_start(out=scratch, in_=gc[:])
@@ -333,14 +334,20 @@ def tile_submatrixlinear_pa_t_kernel(tc, x, scores, Wb, bb, A, B, out):
             elif p0 + 2 >= cnt:
                 nc.sync.dma_start(out=out_v[:, t0 : t0 + cnt, :], in_=ob[:, 0 : cnt * 256].rearrange("p (t o) -> p t o", o=256))
 
-        steps1 = gate_steps(0, GATE_PARTS[0][0], GATE_PARTS[0][1], [])
-        steps2 = gate_steps(1, GATE_PARTS[1][0], GATE_PARTS[1][1], ON_POOL)
-        for f in steps1[0:3]:
+        parts = [gate_steps(n, ta, tb, []) for n, (ta, tb) in enumerate(GATE_PARTS)]
+        for f, g in zip(parts[0], parts[1]):
             f()
-        for f in steps1[3:]:
-            f()
+            g()
+        late_steps = list(zip(parts[2], parts[3]))
+
+        def late_gate_steps(a, b):
+            for f, g in late_steps[a:b]:
+                f()
+                g()
+
+        late_gate_steps(0, 2)
         for k in range(ng):
-            if GROUPS[k][0] < GATE_PARTS[0][1]:
+            if GROUPS[k][0] < 16:
                 emit_X(k)
         if not B_FIRST:
             emit_T(0)
@@ -377,14 +384,12 @@ def tile_submatrixlinear_pa_t_kernel(tc, x, scores, Wb, bb, A, B, out):
                 t_rowtile(bk, Wsb.bitcast(F32), h * 512)
                 c_rowtile(bk, WAg32[:, 0:1024].rearrange("p (g h n u) -> p g h n u", g=2, h=2, u=2)[:, :, h], on_vector=(what in PREP_DVE))
             elif what == "A":
-                A4 = Asb.bitcast(F32).rearrange("p (h m u) -> p h m u", h=2, u=2)
-                for u in range(2):
-                    for h in range(2):
-                        nc.tensor.transpose(bk[:, u * 256 + h * P : u * 256 + (h + 1) * P], A4[:, h, :, u], ident[:])
+                for c in range(4):
+                    nc.tensor.transpose(bk[:, c * P : (c + 1) * P], Ar[:, c * P : (c + 1) * P], ident[:])
                 cp = nc.vector.tensor_copy if what in PREP_DVE else nc.scalar.copy
                 cp(
-                    out=WAg32[:, 1024:1536].rearrange("p (o u) -> p o u", u=2),
-                    in_=bk[:].rearrange("p (u o) -> p o u", u=2),
+                    out=WAg32[:, 1024:1536].rearrange("p (n h u) -> p n h u", h=2, u=2),
+                    in_=bk[:].rearrange("p (u h n) -> p n h u", u=2, h=2),
                 )
             else:
                 nc.tensor.matmul(out=bk[:, 0:256], lhsT=ones[:], rhs=bbz[:], start=True, stop=True)
@@ -393,6 +398,11 @@ def tile_submatrixlinear_pa_t_kernel(tc, x, scores, Wb, bb, A, B, out):
                     out=bb2[:].rearrange("p (r o) -> p r o", r=2),
                     in_=bk[:, 0:256].unsqueeze(1).to_broadcast([P, 2, 256]),
                 )
+
+        def order_A():
+            A5 = Asb.bitcast(F32).rearrange("p (k h m u) -> p u h k m", h=2, m=8, u=2)
+            for u in range(2):
+                nc.scalar.copy(out=Ar[:, u * 256 : (u + 1) * 256].rearrange("p (h k m) -> p h k m", h=2, m=8), in_=A5[:, u])
 
         def quant_piece(what):
             WAg = wag["t"]
@@ -410,7 +420,9 @@ def tile_submatrixlinear_pa_t_kernel(tc, x, scores, Wb, bb, A, B, out):
                 rot["o"] = list(ROT[2]) + list(ROT[0][2:])
             if kt < ng:
                 emit_T(kt)
-            if 0 <= kg < ng and GROUPS[kg][0] < GATE_PARTS[0][1]:
+            if i == 0:
+                emit_Tg(0)
+            if 1 <= kg < ng and GROUPS[kg][0] < 16:
                 emit_Tg(kg)
             if i == TRIP_AT:
                 emit_trip()
@@ -427,13 +439,16 @@ def tile_submatrixlinear_pa_t_kernel(tc, x, scores, Wb, bb, A, B, out):
                         emit_O(ko, p0 + 1, 1)
                     else:
                         emit_O(ko, p0)
+                if i in LATE_MID and p0 == 0:
+                    late_gate_steps(LATE_MID[i][0], LATE_MID[i][1])
             if kt < ng:
                 emit_Q(kt)
             if 0 <= i < ng:
                 emit_Hq(i)
-            if i in GATES2:
-                for f in steps2[GATES2[i][0] : GATES2[i][1]]:
-                    f()
+            if i in LATE_END:
+                late_gate_steps(LATE_END[i][0], LATE_END[i][1])
+            if i == 2:
+                order_A()
             for what in PREP.get(i, []):
                 quant_piece(what)
             if i in LATE_LOADS:

@@ -420,9 +420,7 @@ def tile_submatrixlinear_pa_t_kernel(tc, x, scores, Wb, bb, A, B, out):
                 rot["o"] = list(ROT[2]) + list(ROT[0][2:])
             if kt < ng:
                 emit_T(kt)
-            if i == 0:
-                emit_Tg(0)
-            if 1 <= kg < ng and GROUPS[kg][0] < 16:
+            if 0 <= kg < ng and GROUPS[kg][0] < 16:
                 emit_Tg(kg)
             if i == TRIP_AT:
                 emit_trip()

@@ -418,8 +418,11 @@ def tile_submatrixlinear_pa_t_kernel(tc, x, scores, Wb, bb, A, B, out):
             if kt == ng:
                 rot["u"] = list(ROT[1]) + list(ROT[0][0:2])
                 rot["o"] = list(ROT[2]) + list(ROT[0][2:])
-            if kt < ng:
+            if kt < 9:
                 emit_T(kt)
+            if kt == 9:
+                emit_T(9)
+                emit_T(10)
             if 0 <= kg < ng and GROUPS[kg][0] < 16:
                 emit_Tg(kg)
             if i == TRIP_AT:

@@ -331,8 +331,8 @@ def tile_submatrixlinear_pa_t_kernel(tc, x, scores, Wb, bb, A, B, out):
                     nc.gpsimd.tensor_tensor(out=dst, in0=dst, in1=bb2[:, 0:w], op=ALU.add)
             if wd == 1:
                 nc.sync.dma_start(out=out_v[:, t0 + p0, :], in_=ob[:, p0 * 256 : (p0 + 1) * 256])
-            elif p0 + 2 >= cnt:
-                nc.sync.dma_start(out=out_v[:, t0 : t0 + cnt, :], in_=ob[:, 0 : cnt * 256].rearrange("p (t o) -> p t o", o=256))
+            else:
+                nc.sync.dma_start(out=out_v[:, t0 + p0 : t0 + p0 + 2, :], in_=ob[:, p0 * 256 : p0 * 256 + 512].rearrange("p (t o) -> p t o", o=256))
 
         parts = [gate_steps(n, ta, tb, []) for n, (ta, tb) in enumerate(GATE_PARTS)]
         for f, g in zip(parts[0], parts[1]):

@@ -30,8 +30,8 @@ LATE_MID = {0: (3, 5), 1: (6, 7)}
 LATE_END = {-1: (2, 3), 0: (5, 6), 1: (7, 9)}
 ON_POOL = []
 PREP = {1: ["W0"], 2: ["W1", "bias"], 3: ["A"]}
-LATE_LOADS = {2: 7}
-LOADS = ["sc", (0, 2), "B", (2, 2), (4, 2), (6, 2), "W", "bb", (8, 4), (12, 4), "A", (16, 4), (20, 4), (24, 4)]
+LATE_LOADS = {3: 7}
+LOADS = ["sc", (0, 2), "B", (2, 2), (4, 2), (6, 2), "W", "bb", (8, 4), (12, 4), "A", (16, 4), (20, 4)]
 B_FIRST = False
 SPLIT_LAST = 0
 ROT = ([0, 1, 2, 3], [4, 5], [6, 7])
@@ -233,6 +233,7 @@ def tile_submatrixlinear_pa_t_kernel(tc, x, scores, Wb, bb, A, B, out):
             nc.scalar.copy(out=gc[:], in_=bk[:, 0 : 2 * P])
             scratch = out[0:P, :]
             nc.sync.dma_start(out=scratch, in_=gc[:])
+            load_x(24, 4)
             src = scratch.rearrange("(t k) n -> k t n", k=16)
             for r in range(8):
                 nc.sync.dma_start(out=gT2[r:P:8, :].rearrange("p (t n) -> p t n", n=256), in_=src)
@@ -418,6 +419,8 @@ def tile_submatrixlinear_pa_t_kernel(tc, x, scores, Wb, bb, A, B, out):
             if kt == ng:
                 rot["u"] = list(ROT[1]) + list(ROT[0][0:2])
                 rot["o"] = list(ROT[2]) + list(ROT[0][2:])
+            if i == TRIP_AT:
+                emit_trip()
             if kt < 9:
                 emit_T(kt)
             if kt == 9:
@@ -425,8 +428,6 @@ def tile_submatrixlinear_pa_t_kernel(tc, x, scores, Wb, bb, A, B, out):
                 emit_T(10)
             if 0 <= kg < ng and GROUPS[kg][0] < 16:
                 emit_Tg(kg)
-            if i == TRIP_AT:
-                emit_trip()
             for what in PREP.get(i, []):
                 prep_piece(what)
             nu = GROUPS[i][1] if 0 <= i < ng else 0

@@ -23,6 +23,7 @@ PREP_DVE = []
 CG_DVE = []
 CX_DVE = []
 GATE_PARTS = [(0, 8), (8, 16), (16, 24), (24, 32)]
+WIDE_FROM = 4
 LT = 2
 LO = 4
 TRIP_AT = 3
@@ -48,6 +49,7 @@ def tile_submatrixlinear_pa_t_kernel(tc, x, scores, Wb, bb, A, B, out):
         xg_pool = ctx.enter_context(tc.tile_pool(name="xg", bufs=3))
         xq_pool = ctx.enter_context(tc.tile_pool(name="xq", bufs=LT + LO + 1))
         h_pool = ctx.enter_context(tc.tile_pool(name="h", bufs=2))
+        hw_pool = ctx.enter_context(tc.tile_pool(name="hw", bufs=2))
         hq_pool = ctx.enter_context(tc.tile_pool(name="hq", bufs=LO + 2))
         ob_pool = ctx.enter_context(tc.tile_pool(name="ob", bufs=3))
         psum = ctx.enter_context(tc.psum_pool(name="psum", bufs=1))
@@ -214,7 +216,8 @@ def tile_submatrixlinear_pa_t_kernel(tc, x, scores, Wb, bb, A, B, out):
                 t = t0 + tt
                 bk = bank("tp")
                 t_rowtile(bk, xin[t // 4][:].bitcast(F32), (t % 4) * 512)
-                c_rowtile(bk, xg32[:, tt * 512 : (tt + 1) * 512].rearrange("p (g n u) -> p g n u", g=2, u=2), on_vector=(k in CX_DVE and tt == cnt - 1))
+                pair = xg32[:, (tt // 2) * 1024 : (tt // 2 + 1) * 1024].rearrange("p (g t n u) -> p g t n u", g=2, t=2, u=2)
+                c_rowtile(bk, pair[:, :, tt % 2])
             xgs[k] = xg
 
         def emit_Tg(k):
@@ -249,11 +252,11 @@ def tile_submatrixlinear_pa_t_kernel(tc, x, scores, Wb, bb, A, B, out):
                 )
             xqs[k] = (xq, xs)
 
-        def gate_block(t):
+        def gate_pair(t):
             if t < 16:
-                return gT[:, t * P : (t + 1) * P]
-            b = 2 * ((t - 16) % 8) + (t - 16) // 8
-            return gT2[:, b * P : (b + 1) * P]
+                return gT[:, t * P : (t + 2) * P].rearrange("p (t n) -> p t n", t=2)
+            v = gT2[:].rearrange("p (t c n) -> p c t n", c=2, n=P)
+            return v[:, (t - 16) // 8, (t - 16) % 8 : (t - 16) % 8 + 2]
 
         def emit_U(k, p0):
             t0, cnt = GROUPS[k]
@@ -261,25 +264,49 @@ def tile_submatrixlinear_pa_t_kernel(tc, x, scores, Wb, bb, A, B, out):
             if p0 == 0:
                 hgs[k] = h_pool.tile([P, 2048], BF16, name="hg", tag="hg", align_bytes=256)
             hg = hgs[k]
-            for tt in range(p0, min(p0 + 2, cnt)):
-                t = t0 + tt
+            if k < WIDE_FROM:
+                for tt in range(p0, p0 + 2):
+                    bk = bank("u")
+                    for j in range(4):
+                        for g in range(2):
+                            wc = slice((j * 2 + g) * P, (j * 2 + g + 1) * P)
+                            c0 = p0 * 256 + g * 256 + (tt - p0) * P
+                            nc.tensor.matmul_mx(
+                                out=bk[:, j * P : (j + 1) * P],
+                                lhsT=Bq[:, wc].bitcast(FP8X4), lhsT_scale=Bs[:, wc],
+                                rhs=xq[:, c0 : c0 + P].bitcast(FP8X4), rhs_scale=xs[:, c0 : c0 + P],
+                                start=(g == 0), stop=(g == 1),
+                            )
+                    nc.vector.tensor_tensor(
+                        out=hg[:, tt * 512 : (tt + 1) * 512].rearrange("p (n j) -> p n j", j=4),
+                        in0=bk[:].rearrange("p (j n) -> p n j", j=4),
+                        in1=gate_pair(t0 + p0)[:, tt - p0].unsqueeze(2).to_broadcast([P, P, 4]),
+                        op=ALU.mult,
+                    )
+                return
+            hw = hw_pool.tile([P, 1024], BF16, name="hw", tag="hw", align_bytes=256)
+            for u in range(2):
                 bk = bank("u")
-                for j in range(4):
+                for e in range(2):
                     for g in range(2):
-                        wc = slice((j * 2 + g) * P, (j * 2 + g + 1) * P)
-                        xc = slice((tt * 2 + g) * P, (tt * 2 + g + 1) * P)
+                        wc = slice(((2 * u + e) * 2 + g) * P, ((2 * u + e) * 2 + g + 1) * P)
+                        xc = slice(p0 * 256 + g * 256, p0 * 256 + (g + 1) * 256)
                         nc.tensor.matmul_mx(
-                            out=bk[:, j * P : (j + 1) * P],
+                            out=bk[:, e * 256 : (e + 1) * 256],
                             lhsT=Bq[:, wc].bitcast(FP8X4), lhsT_scale=Bs[:, wc],
                             rhs=xq[:, xc].bitcast(FP8X4), rhs_scale=xs[:, xc],
                             start=(g == 0), stop=(g == 1),
                         )
                 nc.vector.tensor_tensor(
-                    out=hg[:, tt * 512 : (tt + 1) * 512].rearrange("p (n j) -> p n j", j=4),
-                    in0=bk[:].rearrange("p (j n) -> p n j", j=4),
-                    in1=gate_block(t).unsqueeze(2).to_broadcast([P, P, 4]),
+                    out=hw[:, u * 512 : (u + 1) * 512].rearrange("p (t n e) -> p t n e", t=2, e=2),
+                    in0=bk[:].rearrange("p (e t n) -> p t n e", e=2, t=2),
+                    in1=gate_pair(t0 + p0).unsqueeze(3).to_broadcast([P, 2, P, 2]),
                     op=ALU.mult,
                 )
+            nc.scalar.copy(
+                out=hg[:, p0 * 512 : (p0 + 2) * 512].bitcast(F32).rearrange("p (n u) -> p n u", u=2),
+                in_=hw[:].bitcast(F32).rearrange("p (u n) -> p n u", u=2),
+            )
 
         def emit_Hq(k):
             t0, cnt = GROUPS[k]
@@ -309,7 +336,8 @@ def tile_submatrixlinear_pa_t_kernel(tc, x, scores, Wb, bb, A, B, out):
                     tt = p0 + q
                     oc = slice(q * 256, (q + 1) * 256)
                     for g in range(2):
-                        xc = slice((tt * 2 + g) * P, (tt * 2 + g + 1) * P)
+                        c0 = p0 * 256 + g * 256 + (tt - p0) * P
+                        xc = slice(c0, c0 + P)
                         nc.tensor.matmul_mx(
                             out=bk[:, oc],
                             lhsT=xq[:, xc].bitcast(FP8X4), lhsT_scale=xs[:, xc],

@@ -14,30 +14,32 @@ AX = mybir.AxisListType
 
 P = 128
 NT = 32
+HALF = 16
 FLOPS = 2 * 4096 * 1024 * 768 + 2 * 4096 * 512 * 256
 
-MANUAL = True
 GROUPS = [(0, 2), (2, 2), (4, 2), (6, 2), (8, 4), (12, 4), (16, 4), (20, 4), (24, 4), (28, 2), (30, 2)]
-E_DVE = [0, 1, 2, 3, 4, 5, 6, 7, 8, 9, 10]
-PREP_DVE = []
-CG_DVE = []
-CX_DVE = []
-GATE_PARTS = [(0, 8), (8, 16), (16, 24), (24, 32)]
-WIDE_FROM = 4
-LT = 2
-LO = 4
-TRIP_AT = 3
+LOADS = ["sc", (0, 2), "B", (2, 2), (4, 2), (6, 2), "W", "bb", (8, 4), (12, 4), "A", (16, 4), (20, 4)]
+BUNCH = {-1: [1], 0: [2], 1: [3], 2: [4], 3: [5], 4: [6], 5: [7], 6: [8], 7: [9, 10]}
+PREP = {1: ["W0"], 2: ["W1", "bias"], 3: ["A"]}
+GATE_T = {-1: [0], 0: [1], 1: [2], 2: [3], 3: [4], 4: [5]}
 LATE_MID = {0: (3, 5), 1: (6, 7)}
 LATE_END = {-1: (2, 3), 0: (5, 6), 1: (7, 9)}
-ON_POOL = []
-PREP = {1: ["W0"], 2: ["W1", "bias"], 3: ["A"]}
-LATE_LOADS = {3: 7}
-LOADS = ["sc", (0, 2), "B", (2, 2), (4, 2), (6, 2), "W", "bb", (8, 4), (12, 4), "A", (16, 4), (20, 4)]
-B_FIRST = False
-SPLIT_LAST = 0
-ROT = ([0, 1, 2, 3], [4, 5], [6, 7])
-ROUND_ROBIN = True
-LG = 1
+TRIP_AT = 3
+TRIP1 = False
+WIDE = [4, 5, 6, 7, 8, 9, 10]
+O_PAIRS = {4: 1, 5: 1, 6: 1, 7: 1, 8: 2, 9: 2, 10: 2}
+OFFLOAD = []
+X_LATE = False
+ORDER_A = "scalar"
+ORDER_AT = 2
+O_SPLIT_LAST = 0
+XQ_BUFS = 7
+HQ_BUFS = 6
+B_DMAS = 4
+UFIRST = []
+HQE = False
+WARM0 = 0
+WARMB = 0
 
 
 def tile_submatrixlinear_pa_t_kernel(tc, x, scores, Wb, bb, A, B, out):
@@ -47,41 +49,35 @@ def tile_submatrixlinear_pa_t_kernel(tc, x, scores, Wb, bb, A, B, out):
         const = ctx.enter_context(tc.tile_pool(name="const", bufs=1))
         xin_pool = ctx.enter_context(tc.tile_pool(name="xin", bufs=1))
         xg_pool = ctx.enter_context(tc.tile_pool(name="xg", bufs=3))
-        xq_pool = ctx.enter_context(tc.tile_pool(name="xq", bufs=LT + LO + 1))
+        xq_pool = ctx.enter_context(tc.tile_pool(name="xq", bufs=XQ_BUFS))
         h_pool = ctx.enter_context(tc.tile_pool(name="h", bufs=2))
         hw_pool = ctx.enter_context(tc.tile_pool(name="hw", bufs=2))
-        hq_pool = ctx.enter_context(tc.tile_pool(name="hq", bufs=LO + 2))
-        ob_pool = ctx.enter_context(tc.tile_pool(name="ob", bufs=3))
+        hq_pool = ctx.enter_context(tc.tile_pool(name="hq", bufs=HQ_BUFS))
+        ob_pool = ctx.enter_context(tc.tile_pool(name="ob", bufs=8))
         psum = ctx.enter_context(tc.psum_pool(name="psum", bufs=1))
-        if MANUAL:
-            ctx.enter_context(tc.manual_schedule())
+        ctx.enter_context(tc.manual_schedule())
 
-        rot = {"tp": list(ROT[0]), "u": list(ROT[1]), "o": list(ROT[2])}
-        if ROUND_ROBIN:
-            rot["tp"] = [0, 1, 2, 3, 4, 5, 6, 7]
-        cnt_rot = {"tp": 0, "u": 0, "o": 0}
+        used = [0]
 
-        def bank(kind):
-            if ROUND_ROBIN:
-                kind = "tp"
-            b = rot[kind][cnt_rot[kind] % len(rot[kind])]
-            cnt_rot[kind] = cnt_rot[kind] + 1
+        def bank():
+            b = used[0] % 8
+            used[0] = used[0] + 1
             return psum.tile([P, 512], F32, name="bank%d" % b, tag="bank%d" % b)
 
         ident = const.tile([P, P], F32, name="ident")
         ones = const.tile([P, P], BF16, name="ones")
         bbz = const.tile([P, 256], BF16, name="bbz")
-        bb2 = const.tile([P, 512], F32, name="bb2")
+        bb2 = const.tile([P, 256], F32, name="bb2")
         warm = const.tile([P, 1], F32, name="warm")
         sc = const.tile([P, 512], BF16, name="sc")
         gT = const.tile([P, 16 * P], F32, name="gT")
         gT2 = const.tile([P, 16 * P], F32, name="gT2")
         Ar = const.tile([P, 512], F32, name="Ar")
         gc = const.tile([P, 2 * P], F32, name="gc")
+        gc1 = const.tile([P, P], F32, name="gc1")
         Bsb = xin_pool.tile([P, 4096], BF16, name="Bsb", tag="xin7")
-        WAsb = const.tile([P, 3072], BF16, name="WAsb")
-        Wsb = WAsb[:, 0:2048]
-        Asb = WAsb[:, 2048:3072]
+        Wsb = const.tile([P, 2048], BF16, name="Wsb")
+        Asb = const.tile([P, 1024], BF16, name="Asb")
         Bq = const.tile([P, 1024], U32, name="Bq", align_bytes=256)
         Bs = const.tile([P, 1024], U8, name="Bs", align_bytes=256)
         Wq = const.tile([P, 512], U32, name="Wq", align_bytes=256)
@@ -96,59 +92,68 @@ def tile_submatrixlinear_pa_t_kernel(tc, x, scores, Wb, bb, A, B, out):
         nc.vector.memset(bbz[:], 0.0)
         nc.vector.memset(ones[:], 1.0)
         make_identity(nc, ident[:])
+        wz = const.tile([P, 512], BF16, name="wz")
+        if WARM0:
+            nc.gpsimd.memset(wz[:], 0.0)
         nc.scalar.activation(out=warm[:], in_=warm[:], func=ACT.Exp)
 
-        x_v = x.rearrange("(p t) i -> p t i", t=NT)
-        out_v = out.rearrange("(p t) o -> p t o", t=NT)
+        x_v = x.rearrange("(h p t) i -> h p t i", p=P, t=HALF)
+        out_v = out.rearrange("(h p t) o -> h p t o", p=P, t=HALF)
         B_v = B.rearrange("k r i -> (k r) i").rearrange("(p j) i -> p j i", j=4)
 
         def load_x(t0, cnt):
+            if t0 == 28:
+                xin[7] = xin_pool.tile([P, 4096], BF16, name="xin7", tag="xin7")
             dst = xin[t0 // 4][:, (t0 % 4) * 1024 : (t0 % 4 + cnt) * 1024]
-            nc.sync.dma_start(out=dst.rearrange("p (t i) -> p t i", i=1024), in_=x_v[:, t0 : t0 + cnt, :])
+            nc.sync.dma_start(out=dst.rearrange("p (t i) -> p t i", i=1024), in_=x_v[t0 // HALF, :, t0 % HALF : t0 % HALF + cnt, :])
 
-        for item in LOADS:
+        def load(item):
             if item == "sc":
-                nc.sync.dma_start(out=sc[:].rearrange("p (t k) -> p t k", k=16), in_=scores.rearrange("(p t) k -> p t k", t=NT))
+                nc.sync.dma_start(
+                    out=sc[:].rearrange("p (h w) -> p h w", h=2), in_=scores.rearrange("(h p t) k -> p h (t k)", p=P, t=HALF)
+                )
             elif item == "B":
-                for j in range(4):
-                    nc.sync.dma_start(out=Bsb[:, j * 1024 : (j + 1) * 1024], in_=B_v[:, j, :])
+                w = 4 // B_DMAS
+                for j in range(0, 4, w):
+                    nc.sync.dma_start(
+                        out=Bsb[:, j * 1024 : (j + w) * 1024].rearrange("p (j i) -> p j i", i=1024), in_=B_v[:, j : j + w, :]
+                    )
             elif item == "W":
-                nc.sync.dma_start(out=Wsb.rearrange("p (h i) -> p h i", h=2), in_=Wb.rearrange("(h p) i -> p h i", p=P))
+                nc.sync.dma_start(out=Wsb[:].rearrange("p (h i) -> p h i", h=2), in_=Wb.rearrange("(h p) i -> p h i", p=P))
             elif item == "A":
                 nc.sync.dma_start(
-                    out=Asb.rearrange("p (k c) -> p k c", c=64), in_=A.rearrange("k (p h) r -> p k (h r)", h=2)
+                    out=Asb[:].rearrange("p (k c) -> p k c", c=64), in_=A.rearrange("k (p h) r -> p k (h r)", h=2)
                 )
             elif item == "bb":
                 nc.sync.dma_start(out=bbz[0:1, :], in_=bb.rearrange("(o n) -> o n", o=1))
             else:
                 load_x(item[0], item[1])
 
+        for item in LOADS:
+            load(item)
+
         def t_rowtile(bk, src32, col0):
             for c in range(4):
                 nc.tensor.transpose(bk[:, c * P : (c + 1) * P], src32[:, col0 + c * P : col0 + (c + 1) * P], ident[:])
 
-        def c_rowtile(bk, dst, on_vector=False):
-            src = bk[:].rearrange("p (g u n) -> p g n u", g=2, u=2)
-            if on_vector:
-                nc.vector.tensor_copy(out=dst, in_=src)
-            else:
-                nc.scalar.copy(out=dst, in_=src)
+        def c_rowtile(bk, dst):
+            nc.scalar.copy(out=dst, in_=bk[:].rearrange("p (g u n) -> p g n u", g=2, u=2))
 
-        gsrc4 = {}
+        gsrc = {}
         gexps = {}
 
         def emit_X(k):
             t0, cnt = GROUPS[k]
             ge = const.tile([P, cnt * P], F32, name="ge%d" % k)
-            gg, c0 = gsrc4[t0]
+            gg, c0 = gsrc[t0]
             nc.gpsimd.tensor_scalar(
-                out=ge[:, 0 : cnt * P].rearrange("p (c r) -> p c r", r=8),
+                out=ge[:].rearrange("p (c r) -> p c r", r=8),
                 in0=gg[:, c0 : c0 + cnt * 16].unsqueeze(2).to_broadcast([P, cnt * 16, 8]),
                 scalar1=1.0, scalar2=0.0, op0=ALU.mult, op1=ALU.add,
             )
             gexps[k] = ge
 
-        def gate_steps(part, ta, tb, on_pool):
+        def gate_steps(part, ta, tb):
             n = tb - ta
             w = n * 16
             s3 = sc[:, ta * 16 : tb * 16].rearrange("p (t k) -> p t k", k=16)
@@ -161,9 +166,6 @@ def tile_submatrixlinear_pa_t_kernel(tc, x, scores, Wb, bb, A, B, out):
             s1 = const.tile([P, n], F32, name="s1%d" % part)
             r1 = const.tile([P, n], F32, name="r1%d" % part)
             gg = const.tile([P, w], F32, name="gg%d" % part)
-            el_sub = nc.gpsimd if "sub" in on_pool else nc.vector
-            el_thr = nc.gpsimd if "thr" in on_pool else nc.vector
-            el_g = nc.gpsimd if "g" in on_pool else nc.vector
 
             def v3(t):
                 return t[:].rearrange("p (t k) -> p t k", k=16)
@@ -175,7 +177,7 @@ def tile_submatrixlinear_pa_t_kernel(tc, x, scores, Wb, bb, A, B, out):
                 nc.vector.tensor_reduce(out=mx[:], in_=s3, axis=AX.X, op=ALU.max)
 
             def st_sub():
-                el_sub.tensor_tensor(out=v3(dd), in0=s3, in1=b3(mx), op=ALU.subtract)
+                nc.vector.tensor_tensor(out=v3(dd), in0=s3, in1=b3(mx), op=ALU.subtract)
 
             def st_exp():
                 nc.scalar.activation(out=ee[:], in_=dd[:], func=ACT.Exp)
@@ -187,7 +189,7 @@ def tile_submatrixlinear_pa_t_kernel(tc, x, scores, Wb, bb, A, B, out):
                 nc.vector.scalar_tensor_tensor(out=v3(g0), in0=v3(ee), scalar=20.0, in1=b3(ss), op0=ALU.mult, op1=ALU.is_gt)
 
             def st_thr():
-                el_thr.tensor_tensor(out=g1[:], in0=g0[:], in1=ee[:], op=ALU.mult)
+                nc.vector.tensor_tensor(out=g1[:], in0=g0[:], in1=ee[:], op=ALU.mult)
 
             def st_sum1():
                 nc.vector.tensor_reduce(out=s1[:], in_=v3(g1), axis=AX.X, op=ALU.add)
@@ -196,17 +198,17 @@ def tile_submatrixlinear_pa_t_kernel(tc, x, scores, Wb, bb, A, B, out):
                 nc.vector.reciprocal(out=r1[:], in_=s1[:])
 
             def st_g():
-                el_g.tensor_tensor(out=v3(gg), in0=v3(g1), in1=b3(r1), op=ALU.mult)
+                nc.vector.tensor_tensor(out=v3(gg), in0=v3(g1), in1=b3(r1), op=ALU.mult)
 
             for t in range(ta, tb):
-                gsrc4[t] = (gg, (t - ta) * 16)
+                gsrc[t] = (gg, (t - ta) * 16)
             return [st_max, st_sub, st_exp, st_sum, st_g0, st_thr, st_sum1, st_rec, st_g]
 
         xgs = {}
         xqs = {}
         hgs = {}
         hqs = {}
-        obs = {}
+        late_stores = []
 
         def emit_T(k):
             t0, cnt = GROUPS[k]
@@ -214,7 +216,7 @@ def tile_submatrixlinear_pa_t_kernel(tc, x, scores, Wb, bb, A, B, out):
             xg32 = xg[:].bitcast(F32)
             for tt in range(cnt):
                 t = t0 + tt
-                bk = bank("tp")
+                bk = bank()
                 t_rowtile(bk, xin[t // 4][:].bitcast(F32), (t % 4) * 512)
                 pair = xg32[:, (tt // 2) * 1024 : (tt // 2 + 1) * 1024].rearrange("p (g t n u) -> p g t n u", g=2, t=2, u=2)
                 c_rowtile(bk, pair[:, :, tt % 2])
@@ -222,34 +224,49 @@ def tile_submatrixlinear_pa_t_kernel(tc, x, scores, Wb, bb, A, B, out):
 
         def emit_Tg(k):
             t0, cnt = GROUPS[k]
-            bk = bank("tp")
+            bk = bank()
             for tt in range(cnt):
-                t = t0 + tt
                 nc.tensor.transpose(bk[:, tt * P : (tt + 1) * P], gexps[k][:, tt * P : (tt + 1) * P], ident[:])
-            cp = nc.vector.tensor_copy if k in CG_DVE else nc.scalar.copy
-            cp(out=gT[:, t0 * P : (t0 + cnt) * P], in_=bk[:, 0 : cnt * P])
+            nc.scalar.copy(out=gT[:, t0 * P : (t0 + cnt) * P], in_=bk[:, 0 : cnt * P])
 
         def emit_trip():
-            bk = bank("tp")
+            bk = bank()
             for c in range(2):
-                nc.tensor.transpose(bk[:, c * P : (c + 1) * P], gsrc4[16 + 8 * c][0][:], ident[:])
+                nc.tensor.transpose(bk[:, c * P : (c + 1) * P], gsrc[16][0][:, c * P : (c + 1) * P], ident[:])
             nc.scalar.copy(out=gc[:], in_=bk[:, 0 : 2 * P])
-            scratch = out[0:P, :]
-            nc.sync.dma_start(out=scratch, in_=gc[:])
+            scratch = out[3072:4096, :]
+            nc.sync.dma_start(
+                out=scratch.rearrange("(q r) n -> q r n", r=8), in_=gc[:].unsqueeze(1).to_broadcast([P, 8, 256])
+            )
             load_x(24, 4)
-            src = scratch.rearrange("(t k) n -> k t n", k=16)
-            for r in range(8):
-                nc.sync.dma_start(out=gT2[r:P:8, :].rearrange("p (t n) -> p t n", n=256), in_=src)
+            nc.sync.dma_start(
+                out=gT2[:].rearrange("p (t n) -> p t n", n=256), in_=scratch.rearrange("(t q) n -> q t n", q=P)
+            )
+            load_x(28, 4)
+
+        def emit_trip1():
+            bk = bank()
+            nc.tensor.transpose(bk[:, 0:P], gsrc[8][0][:], ident[:])
+            nc.scalar.copy(out=gc1[:], in_=bk[:, 0:P])
+            scratch = out[2048:3072, 0:P]
+            nc.sync.dma_start(
+                out=scratch.rearrange("(q r) n -> q r n", r=8), in_=gc1[:].unsqueeze(1).to_broadcast([P, 8, P])
+            )
+            load_x(12, 4)
+            nc.sync.dma_start(
+                out=gT[:, 8 * P : 16 * P].rearrange("p (t n) -> p t n", n=P), in_=scratch.rearrange("(t q) n -> q t n", q=P)
+            )
+            load("A")
+            load_x(16, 4)
+            load_x(20, 4)
 
         def emit_Q(k):
             t0, cnt = GROUPS[k]
             xq = xq_pool.tile([P, 1024], U32, name="xq", tag="xq", align_bytes=256)
             xs = xq_pool.tile([P, 1024], U8, name="xs", tag="xs", align_bytes=256)
-            for a, n in ([(0, 2), (2, 1)] if cnt == 3 else [(0, cnt)]):
-                nc.vector.quantize_mx(
-                    out=xq[:, a * 256 : (a + n) * 256].bitcast(FP8X4), scales=xs[:, a * 256 : (a + n) * 256],
-                    in_=xgs[k][:, a * 1024 : (a + n) * 1024],
-                )
+            nc.vector.quantize_mx(
+                out=xq[:, 0 : cnt * 256].bitcast(FP8X4), scales=xs[:, 0 : cnt * 256], in_=xgs[k][:, 0 : cnt * 1024]
+            )
             xqs[k] = (xq, xs)
 
         def gate_pair(t):
@@ -264,9 +281,9 @@ def tile_submatrixlinear_pa_t_kernel(tc, x, scores, Wb, bb, A, B, out):
             if p0 == 0:
                 hgs[k] = h_pool.tile([P, 2048], BF16, name="hg", tag="hg", align_bytes=256)
             hg = hgs[k]
-            if k < WIDE_FROM:
+            if k not in WIDE:
                 for tt in range(p0, p0 + 2):
-                    bk = bank("u")
+                    bk = bank()
                     for j in range(4):
                         for g in range(2):
                             wc = slice((j * 2 + g) * P, (j * 2 + g + 1) * P)
@@ -286,7 +303,7 @@ def tile_submatrixlinear_pa_t_kernel(tc, x, scores, Wb, bb, A, B, out):
                 return
             hw = hw_pool.tile([P, 1024], BF16, name="hw", tag="hw", align_bytes=256)
             for u in range(2):
-                bk = bank("u")
+                bk = bank()
                 for e in range(2):
                     for g in range(2):
                         wc = slice(((2 * u + e) * 2 + g) * P, ((2 * u + e) * 2 + g + 1) * P)
@@ -312,126 +329,130 @@ def tile_submatrixlinear_pa_t_kernel(tc, x, scores, Wb, bb, A, B, out):
             t0, cnt = GROUPS[k]
             hq = hq_pool.tile([P, 512], U32, name="hq", tag="hq", align_bytes=256)
             hs = hq_pool.tile([P, 512], U8, name="hs", tag="hs", align_bytes=256)
-            for a, n in ([(0, 2), (2, 1)] if cnt == 3 else [(0, cnt)]):
-                nc.vector.quantize_mx(
-                    out=hq[:, a * P : (a + n) * P].bitcast(FP8X4), scales=hs[:, a * P : (a + n) * P],
-                    in_=hgs[k][:, a * 512 : (a + n) * 512],
-                )
+            nc.vector.quantize_mx(
+                out=hq[:, 0 : cnt * P].bitcast(FP8X4), scales=hs[:, 0 : cnt * P], in_=hgs[k][:, 0 : cnt * 512]
+            )
             hqs[k] = (hq, hs)
 
-        def emit_O(k, p0, wd=2):
+        def emit_O(k, p0):
             t0, cnt = GROUPS[k]
             xq, xs = xqs[k]
             hq, hs = hqs[k]
-            if p0 == 0:
-                if cnt >= 3:
-                    obs[k] = ob_pool.tile([P, 1024], F32, name="ob", tag="ob")
-                else:
-                    obs[k] = ob_pool.tile([P, 512], F32, name="obs", tag="obs")
-            ob = obs[k]
-            if True:
-                np_ = min(wd, cnt - p0)
-                bk = bank("o")
-                for q in range(np_):
-                    tt = p0 + q
-                    oc = slice(q * 256, (q + 1) * 256)
-                    for g in range(2):
-                        c0 = p0 * 256 + g * 256 + (tt - p0) * P
-                        xc = slice(c0, c0 + P)
-                        nc.tensor.matmul_mx(
-                            out=bk[:, oc],
-                            lhsT=xq[:, xc].bitcast(FP8X4), lhsT_scale=xs[:, xc],
-                            rhs=Wq[:, g * 256 : (g + 1) * 256].bitcast(FP8X4), rhs_scale=Ws[:, g * 256 : (g + 1) * 256],
-                            start=(g == 0), stop=False,
-                        )
-                    hc = slice(tt * P, (tt + 1) * P)
+            bk = bank()
+            for q in range(2):
+                oc = slice(q * 256, (q + 1) * 256)
+                for g in range(2):
+                    c0 = p0 * 256 + g * 256 + q * P
                     nc.tensor.matmul_mx(
                         out=bk[:, oc],
-                        lhsT=hq[:, hc].bitcast(FP8X4), lhsT_scale=hs[:, hc],
-                        rhs=Aq[:].bitcast(FP8X4), rhs_scale=As[:],
-                        start=False, stop=True,
+                        lhsT=xq[:, c0 : c0 + P].bitcast(FP8X4), lhsT_scale=xs[:, c0 : c0 + P],
+                        rhs=Wq[:, g * 256 : (g + 1) * 256].bitcast(FP8X4), rhs_scale=Ws[:, g * 256 : (g + 1) * 256],
+                        start=(g == 0), stop=False,
                     )
-                w = np_ * 256
-                dst = ob[:, p0 * 256 : p0 * 256 + w]
-                if k in E_DVE:
-                    nc.vector.tensor_tensor(out=dst, in0=bk[:, 0:w], in1=bb2[:, 0:w], op=ALU.add)
-                else:
-                    nc.scalar.copy(out=dst, in_=bk[:, 0:w])
-                    nc.gpsimd.tensor_tensor(out=dst, in0=dst, in1=bb2[:, 0:w], op=ALU.add)
-            if wd == 1:
-                nc.sync.dma_start(out=out_v[:, t0 + p0, :], in_=ob[:, p0 * 256 : (p0 + 1) * 256])
-            else:
-                nc.sync.dma_start(out=out_v[:, t0 + p0 : t0 + p0 + 2, :], in_=ob[:, p0 * 256 : p0 * 256 + 512].rearrange("p (t o) -> p t o", o=256))
+                hc = slice((p0 + q) * P, (p0 + q + 1) * P)
+                nc.tensor.matmul_mx(
+                    out=bk[:, oc],
+                    lhsT=hq[:, hc].bitcast(FP8X4), lhsT_scale=hs[:, hc],
+                    rhs=Aq[:].bitcast(FP8X4), rhs_scale=As[:],
+                    start=False, stop=True,
+                )
+            ob = ob_pool.tile([P, 512], F32, name="ob", tag="ob")
+            o3 = ob[:].rearrange("p (t o) -> p t o", o=256)
+            b3 = bb2[:].unsqueeze(1).to_broadcast([P, 2, 256])
+            t = t0 + p0
+            dram = out_v[t // HALF, :, t % HALF : t % HALF + 2, :]
 
-        parts = [gate_steps(n, ta, tb, []) for n, (ta, tb) in enumerate(GATE_PARTS)]
-        for f, g in zip(parts[0], parts[1]):
+            def store():
+                nc.sync.dma_start(out=dram, in_=o3)
+
+            if (k, p0) in OFFLOAD:
+                nc.scalar.copy(out=ob[:], in_=bk[:])
+                nc.gpsimd.tensor_tensor(out=o3, in0=o3, in1=b3, op=ALU.add)
+                late_stores.append(store)
+            else:
+                nc.vector.tensor_tensor(out=o3, in0=bk[:].rearrange("p (t o) -> p t o", o=256), in1=b3, op=ALU.add)
+                store()
+                while late_stores:
+                    late_stores.pop(0)()
+
+        parts = [gate_steps(n, ta, tb) for n, (ta, tb) in enumerate([(0, 8), (8, 16), (16, 32)])]
+        for n, f in enumerate(parts[0]):
             f()
-            g()
-        late_steps = list(zip(parts[2], parts[3]))
+            if not X_LATE or n < 8:
+                parts[1][n]()
+        late_steps = parts[2]
 
         def late_gate_steps(a, b):
-            for f, g in late_steps[a:b]:
+            for f in late_steps[a:b]:
                 f()
-                g()
 
         late_gate_steps(0, 2)
         for k in range(ng):
-            if GROUPS[k][0] < 16:
+            if GROUPS[k][0] < 8:
                 emit_X(k)
-        if not B_FIRST:
-            emit_T(0)
+        if not X_LATE and not TRIP1:
+            emit_X(4)
+            emit_X(5)
+        def warm_up(n):
+            if n:
+                bk = bank()
+                for m in range(n):
+                    nc.tensor.matmul(out=bk[:], lhsT=wz[:, 0:P], rhs=wz[:], start=True, stop=True)
+
+        warm_up(WARM0)
+        emit_T(0)
         Bg = xg_pool.tile([P, 4096], BF16, name="Bg", tag="xg", align_bytes=256)
         Bg32 = Bg[:].bitcast(F32)
-        Bsb32 = Bsb[:].bitcast(F32)
         for j in range(4):
-            bk = bank("tp")
-            t_rowtile(bk, Bsb32, j * 512)
+            bk = bank()
+            if WARMB and j:
+                warm_up(WARMB)
+                bk = bank()
+            t_rowtile(bk, Bsb[:].bitcast(F32), j * 512)
             c_rowtile(bk, Bg32[:, j * 512 : (j + 1) * 512].rearrange("p (g n u) -> p g n u", g=2, u=2))
-        if B_FIRST:
-            emit_T(0)
-        else:
-            emit_Q(0)
+        emit_Q(0)
         for hf in range(2):
             nc.vector.quantize_mx(
                 out=Bq[:, hf * 512 : (hf + 1) * 512].bitcast(FP8X4),
                 scales=Bs[:, hf * 512 : (hf + 1) * 512],
                 in_=Bg[:, hf * 2048 : (hf + 1) * 2048],
             )
-        if B_FIRST:
-            emit_Q(0)
+        if X_LATE:
+            parts[1][8]()
+            if not TRIP1:
+                emit_X(4)
+                emit_X(5)
 
         wag = {}
 
         def prep_piece(what):
             if "t" not in wag:
                 wag["t"] = xg_pool.tile([P, 3072], BF16, name="WAg", tag="wag", bufs=1, align_bytes=256)
-            WAg = wag["t"]
-            WAg32 = WAg[:].bitcast(F32)
-            bk = bank("tp")
+            WAg32 = wag["t"][:].bitcast(F32)
+            bk = bank()
             if what == "W0" or what == "W1":
                 h = 0 if what == "W0" else 1
-                t_rowtile(bk, Wsb.bitcast(F32), h * 512)
-                c_rowtile(bk, WAg32[:, 0:1024].rearrange("p (g h n u) -> p g h n u", g=2, h=2, u=2)[:, :, h], on_vector=(what in PREP_DVE))
+                t_rowtile(bk, Wsb[:].bitcast(F32), h * 512)
+                c_rowtile(bk, WAg32[:, 0:1024].rearrange("p (g h n u) -> p g h n u", g=2, h=2, u=2)[:, :, h])
             elif what == "A":
                 for c in range(4):
                     nc.tensor.transpose(bk[:, c * P : (c + 1) * P], Ar[:, c * P : (c + 1) * P], ident[:])
-                cp = nc.vector.tensor_copy if what in PREP_DVE else nc.scalar.copy
-                cp(
+                nc.scalar.copy(
                     out=WAg32[:, 1024:1536].rearrange("p (n h u) -> p n h u", h=2, u=2),
                     in_=bk[:].rearrange("p (u h n) -> p n h u", u=2, h=2),
                 )
             else:
                 nc.tensor.matmul(out=bk[:, 0:256], lhsT=ones[:], rhs=bbz[:], start=True, stop=True)
-                cp = nc.vector.tensor_copy if what in PREP_DVE else nc.scalar.copy
-                cp(
-                    out=bb2[:].rearrange("p (r o) -> p r o", r=2),
-                    in_=bk[:, 0:256].unsqueeze(1).to_broadcast([P, 2, 256]),
-                )
+                nc.scalar.copy(out=bb2[:], in_=bk[:, 0:256])
 
         def order_A():
-            A5 = Asb.bitcast(F32).rearrange("p (k h m u) -> p u h k m", h=2, m=8, u=2)
+            A5 = Asb[:].bitcast(F32).rearrange("p (k h m u) -> p u h k m", h=2, m=8, u=2)
             for u in range(2):
-                nc.scalar.copy(out=Ar[:, u * 256 : (u + 1) * 256].rearrange("p (h k m) -> p h k m", h=2, m=8), in_=A5[:, u])
+                dst = Ar[:, u * 256 : (u + 1) * 256].rearrange("p (h k m) -> p h k m", h=2, m=8)
+                if ORDER_A == "scalar":
+                    nc.scalar.copy(out=dst, in_=A5[:, u])
+                else:
+                    nc.vector.tensor_copy(out=dst, in_=A5[:, u])
 
         def quant_piece(what):
             WAg = wag["t"]
@@ -440,48 +461,42 @@ def tile_submatrixlinear_pa_t_kernel(tc, x, scores, Wb, bb, A, B, out):
             if what == "A":
                 nc.vector.quantize_mx(out=Aq[:].bitcast(FP8X4), scales=As[:], in_=WAg[:, 2048:3072])
 
-        for i in range(1 - LT, ng + LO):
-            kt = i + LT
-            kg = i + LG
-            ko = i - LO
-            if kt == ng:
-                rot["u"] = list(ROT[1]) + list(ROT[0][0:2])
-                rot["o"] = list(ROT[2]) + list(ROT[0][2:])
+        o_pairs = [(k, p0) for k in range(ng) for p0 in range(0, GROUPS[k][1], 2)]
+        for i in range(-1, ng + 1):
+            if i in UFIRST:
+                for p0 in range(0, GROUPS[i][1], 2):
+                    emit_U(i, p0)
             if i == TRIP_AT:
                 emit_trip()
-            if kt < 9:
-                emit_T(kt)
-            if kt == 9:
-                emit_T(9)
-                emit_T(10)
-            if 0 <= kg < ng and GROUPS[kg][0] < 16:
-                emit_Tg(kg)
+            for k in BUNCH.get(i, []):
+                emit_T(k)
+            for k in GATE_T.get(i, []):
+                if not (TRIP1 and GROUPS[k][0] >= 8):
+                    emit_Tg(k)
+            if TRIP1 and i == 0:
+                emit_trip1()
             for what in PREP.get(i, []):
                 prep_piece(what)
-            nu = GROUPS[i][1] if 0 <= i < ng else 0
-            no = GROUPS[ko][1] if 0 <= ko < ng else 0
-            for p0 in range(0, max(nu, no), 2):
-                if p0 < nu:
-                    emit_U(i, p0)
-                if p0 < no:
-                    if ko >= ng - SPLIT_LAST:
-                        emit_O(ko, p0, 1)
-                        emit_O(ko, p0 + 1, 1)
-                    else:
-                        emit_O(ko, p0)
-                if i in LATE_MID and p0 == 0:
+            nu = GROUPS[i][1] // 2 if 0 <= i < ng and i not in UFIRST else 0
+            no = len(o_pairs) if i >= ng else O_PAIRS.get(i, 0)
+            for n in range(max(nu, no)):
+                if n < nu:
+                    emit_U(i, 2 * n)
+                    if i == ng - 1 and HQE:
+                        emit_Hq(i)
+                if n < no:
+                    emit_O(*o_pairs.pop(0))
+                if i in LATE_MID and n == 0:
                     late_gate_steps(LATE_MID[i][0], LATE_MID[i][1])
-            if kt < ng:
-                emit_Q(kt)
-            if 0 <= i < ng:
+            for k in BUNCH.get(i, []):
+                emit_Q(k)
+            if 0 <= i < ng and not (HQE and i == ng - 1):
                 emit_Hq(i)
             if i in LATE_END:
                 late_gate_steps(LATE_END[i][0], LATE_END[i][1])
-            if i == 2:
+            if i == ORDER_AT:
                 order_A()
             for what in PREP.get(i, []):
                 quant_piece(what)
-            if i in LATE_LOADS:
-                d = LATE_LOADS[i]
-                xin[d] = xin_pool.tile([P, 4096], BF16, name="xin%d" % d, tag="xin%d" % d)
-                load_x(4 * d, 4)
+        while late_stores:
+            late_stores.pop(0)()

@@ -26,10 +26,10 @@ LATE_MID = {0: (3, 5), 1: (6, 7)}
 LATE_END = {-1: (2, 3), 0: (5, 6), 1: (7, 9)}
 TRIP_AT = 3
 TRIP1 = False
-WIDE = [4, 5, 6, 7, 8, 9, 10]
-O_PAIRS = {4: 1, 5: 1, 6: 1, 7: 1, 8: 2, 9: 2, 10: 2}
+WIDE = [4, 5, 6, 7, 8, 9]
+O_PAIRS = {4: 1, 5: 1, 6: 1, 7: 1, 8: 3, 9: 3, 10: 2}
 OFFLOAD = []
-X_LATE = False
+X_LATE = True
 ORDER_A = "scalar"
 ORDER_AT = 2
 O_SPLIT_LAST = 0
@@ -38,8 +38,8 @@ HQ_BUFS = 6
 B_DMAS = 4
 UFIRST = []
 HQE = False
-WARM0 = 0
-WARMB = 0
+WARM0 = 6
+WARMB = 2
 
 
 def tile_submatrixlinear_pa_t_kernel(tc, x, scores, Wb, bb, A, B, out):
@@ -470,6 +470,8 @@ def tile_submatrixlinear_pa_t_kernel(tc, x, scores, Wb, bb, A, B, out):
                 emit_trip()
             for k in BUNCH.get(i, []):
                 emit_T(k)
+            if i == -1:
+                warm_up(WARMB)
             for k in GATE_T.get(i, []):
                 if not (TRIP1 and GROUPS[k][0] >= 8):
                     emit_Tg(k)

@@ -21,25 +21,36 @@ GROUPS = [(0, 2), (2, 2), (4, 2), (6, 2), (8, 4), (12, 4), (16, 4), (20, 4), (24
 LOADS = ["sc", (0, 2), "B", (2, 2), (4, 2), (6, 2), "W", "bb", (8, 4), (12, 4), "A", (16, 4), (20, 4)]
 BUNCH = {-1: [1], 0: [2], 1: [3], 2: [4], 3: [5], 4: [6], 5: [7], 6: [8], 7: [9, 10]}
 PREP = {1: ["W0"], 2: ["W1", "bias"], 3: ["A"]}
-GATE_T = {-1: [0], 0: [1], 1: [2], 2: [3], 3: [4], 4: [5]}
+GATE_T = {-1: [0], 0: [1], 1: [2, 3, 4, 5]}
 LATE_MID = {0: (3, 5), 1: (6, 7)}
 LATE_END = {-1: (2, 3), 0: (5, 6), 1: (7, 9)}
 TRIP_AT = 3
 TRIP1 = False
 WIDE = [4, 5, 6, 7, 8, 9]
 O_PAIRS = {4: 1, 5: 1, 6: 1, 7: 1, 8: 3, 9: 3, 10: 2}
-OFFLOAD = []
-X_LATE = True
+OFFLOAD = [(4, 0), (5, 0), (6, 0)]
+X_LATE = False
 ORDER_A = "scalar"
 ORDER_AT = 2
 O_SPLIT_LAST = 0
 XQ_BUFS = 7
 HQ_BUFS = 6
-B_DMAS = 4
+B_DMAS = 2
 UFIRST = []
+TRIP_Q = "sync"
+PE_TILES = 16
+Q_MID = []
+X45_AT = -9
+HEAD = ["gates", "L0", "L1", "X", "T0", "B0", "B1", "B2", "B3", "Q0", "QB02", "QB24", "G", "X45"]
+SPLIT = []
+CHUNK = 1
+TRIP_MID = [24]
+TRIP_END = [28]
+X67_AT = 2
+READ_AT = 4
 HQE = False
-WARM0 = 6
-WARMB = 2
+WARM0 = 0
+WARMB = 0
 
 
 def tile_submatrixlinear_pa_t_kernel(tc, x, scores, Wb, bb, A, B, out):
@@ -70,10 +81,10 @@ def tile_submatrixlinear_pa_t_kernel(tc, x, scores, Wb, bb, A, B, out):
         bb2 = const.tile([P, 256], F32, name="bb2")
         warm = const.tile([P, 1], F32, name="warm")
         sc = const.tile([P, 512], BF16, name="sc")
-        gT = const.tile([P, 16 * P], F32, name="gT")
-        gT2 = const.tile([P, 16 * P], F32, name="gT2")
+        gT = const.tile([P, PE_TILES * P], F32, name="gT")
+        gT2 = const.tile([P, (32 - PE_TILES) * P], F32, name="gT2")
         Ar = const.tile([P, 512], F32, name="Ar")
-        gc = const.tile([P, 2 * P], F32, name="gc")
+        gc = const.tile([P, (32 - PE_TILES) * 16], F32, name="gc")
         gc1 = const.tile([P, P], F32, name="gc1")
         Bsb = xin_pool.tile([P, 4096], BF16, name="Bsb", tag="xin7")
         Wsb = const.tile([P, 2048], BF16, name="Wsb")
@@ -119,7 +130,7 @@ def tile_submatrixlinear_pa_t_kernel(tc, x, scores, Wb, bb, A, B, out):
                         out=Bsb[:, j * 1024 : (j + w) * 1024].rearrange("p (j i) -> p j i", i=1024), in_=B_v[:, j : j + w, :]
                     )
             elif item == "W":
-                nc.sync.dma_start(out=Wsb[:].rearrange("p (h i) -> p h i", h=2), in_=Wb.rearrange("(h p) i -> p h i", p=P))
+                nc.sync.dma_start(out=Wsb[:], in_=Wb.rearrange("(p h) i -> p (h i)", h=2))
             elif item == "A":
                 nc.sync.dma_start(
                     out=Asb[:].rearrange("p (k c) -> p k c", c=64), in_=A.rearrange("k (p h) r -> p k (h r)", h=2)
@@ -229,20 +240,31 @@ def tile_submatrixlinear_pa_t_kernel(tc, x, scores, Wb, bb, A, B, out):
                 nc.tensor.transpose(bk[:, tt * P : (tt + 1) * P], gexps[k][:, tt * P : (tt + 1) * P], ident[:])
             nc.scalar.copy(out=gT[:, t0 * P : (t0 + cnt) * P], in_=bk[:, 0 : cnt * P])
 
+        def emit_trip_read():
+            q = nc.scalar if TRIP_Q == "scalar" else nc.sync
+            q.dma_start(
+                out=gT2[:].rearrange("p (t n) -> p t n", t=8), in_=out[3072:4096, 0 : (32 - PE_TILES) * 16].rearrange("(t q) n -> q t n", q=P)
+            )
+
         def emit_trip():
             bk = bank()
-            for c in range(2):
-                nc.tensor.transpose(bk[:, c * P : (c + 1) * P], gsrc[16][0][:, c * P : (c + 1) * P], ident[:])
-            nc.scalar.copy(out=gc[:], in_=bk[:, 0 : 2 * P])
-            scratch = out[3072:4096, :]
-            nc.sync.dma_start(
-                out=scratch.rearrange("(q r) n -> q r n", r=8), in_=gc[:].unsqueeze(1).to_broadcast([P, 8, 256])
+            nb = (32 - PE_TILES) // 8
+            for c in range(nb):
+                c0 = (PE_TILES - 16) * 16 + c * P
+                nc.tensor.transpose(bk[:, c * P : (c + 1) * P], gsrc[16][0][:, c0 : c0 + P], ident[:])
+            nc.scalar.copy(out=gc[:], in_=bk[:, 0 : nb * P])
+            q = nc.scalar if TRIP_Q == "scalar" else nc.sync
+            q.dma_start(
+                out=out[3072:4096, 0 : (32 - PE_TILES) * 16].rearrange("(q r) n -> q r n", r=8), in_=gc[:].unsqueeze(1).to_broadcast([P, 8, (32 - PE_TILES) * 16])
             )
-            load_x(24, 4)
-            nc.sync.dma_start(
-                out=gT2[:].rearrange("p (t n) -> p t n", n=256), in_=scratch.rearrange("(t q) n -> q t n", q=P)
-            )
-            load_x(28, 4)
+            if TRIP_Q == "sync":
+                for t0 in TRIP_MID:
+                    load_x(t0, 4)
+                emit_trip_read()
+                for t0 in TRIP_END:
+                    load_x(t0, 4)
+            else:
+                load_x(28, 4)
 
         def emit_trip1():
             bk = bank()
@@ -270,10 +292,10 @@ def tile_submatrixlinear_pa_t_kernel(tc, x, scores, Wb, bb, A, B, out):
             xqs[k] = (xq, xs)
 
         def gate_pair(t):
-            if t < 16:
+            if t < PE_TILES:
                 return gT[:, t * P : (t + 2) * P].rearrange("p (t n) -> p t n", t=2)
-            v = gT2[:].rearrange("p (t c n) -> p c t n", c=2, n=P)
-            return v[:, (t - 16) // 8, (t - 16) % 8 : (t - 16) % 8 + 2]
+            v = gT2[:].rearrange("p (t c n) -> p c t n", t=8, n=P)
+            return v[:, (t - PE_TILES) // 8, t % 8 : t % 8 + 2]
 
         def emit_U(k, p0):
             t0, cnt = GROUPS[k]
@@ -338,9 +360,12 @@ def tile_submatrixlinear_pa_t_kernel(tc, x, scores, Wb, bb, A, B, out):
             t0, cnt = GROUPS[k]
             xq, xs = xqs[k]
             hq, hs = hqs[k]
+            split = (k, p0) in SPLIT
             bk = bank()
+            bks = [bk, bank()] if split else [bk, bk]
             for q in range(2):
-                oc = slice(q * 256, (q + 1) * 256)
+                bk = bks[q]
+                oc = slice(0, 256) if split else slice(q * 256, (q + 1) * 256)
                 for g in range(2):
                     c0 = p0 * 256 + g * 256 + q * P
                     nc.tensor.matmul_mx(
@@ -356,6 +381,13 @@ def tile_submatrixlinear_pa_t_kernel(tc, x, scores, Wb, bb, A, B, out):
                     rhs=Aq[:].bitcast(FP8X4), rhs_scale=As[:],
                     start=False, stop=True,
                 )
+                if split:
+                    ob = ob_pool.tile([P, 512], F32, name="ob", tag="ob")
+                    nc.vector.tensor_tensor(out=ob[:, 0:256], in0=bk[:, 0:256], in1=bb2[:], op=ALU.add)
+                    t = t0 + p0 + q
+                    nc.sync.dma_start(out=out_v[t // HALF, :, t % HALF, :], in_=ob[:, 0:256])
+            if split:
+                return
             ob = ob_pool.tile([P, 512], F32, name="ob", tag="ob")
             o3 = ob[:].rearrange("p (t o) -> p t o", o=256)
             b3 = bb2[:].unsqueeze(1).to_broadcast([P, 2, 256])
@@ -367,7 +399,12 @@ def tile_submatrixlinear_pa_t_kernel(tc, x, scores, Wb, bb, A, B, out):
 
             if (k, p0) in OFFLOAD:
                 nc.scalar.copy(out=ob[:], in_=bk[:])
-                nc.gpsimd.tensor_tensor(out=o3, in0=o3, in1=b3, op=ALU.add)
+                w = 512 // CHUNK
+                for c in range(0, 512, w):
+                    if w > 256:
+                        nc.gpsimd.tensor_tensor(out=o3, in0=o3, in1=b3, op=ALU.add)
+                    else:
+                        nc.gpsimd.tensor_tensor(out=ob[:, c : c + w], in0=ob[:, c : c + w], in1=bb2[:, c % 256 : c % 256 + w], op=ALU.add)
                 late_stores.append(store)
             else:
                 nc.vector.tensor_tensor(out=o3, in0=bk[:].rearrange("p (t o) -> p t o", o=256), in1=b3, op=ALU.add)
@@ -376,23 +413,12 @@ def tile_submatrixlinear_pa_t_kernel(tc, x, scores, Wb, bb, A, B, out):
                     late_stores.pop(0)()
 
         parts = [gate_steps(n, ta, tb) for n, (ta, tb) in enumerate([(0, 8), (8, 16), (16, 32)])]
-        for n, f in enumerate(parts[0]):
-            f()
-            if not X_LATE or n < 8:
-                parts[1][n]()
         late_steps = parts[2]
 
         def late_gate_steps(a, b):
             for f in late_steps[a:b]:
                 f()
 
-        late_gate_steps(0, 2)
-        for k in range(ng):
-            if GROUPS[k][0] < 8:
-                emit_X(k)
-        if not X_LATE and not TRIP1:
-            emit_X(4)
-            emit_X(5)
         def warm_up(n):
             if n:
                 bk = bank()
@@ -400,28 +426,51 @@ def tile_submatrixlinear_pa_t_kernel(tc, x, scores, Wb, bb, A, B, out):
                     nc.tensor.matmul(out=bk[:], lhsT=wz[:, 0:P], rhs=wz[:], start=True, stop=True)
 
         warm_up(WARM0)
-        emit_T(0)
         Bg = xg_pool.tile([P, 4096], BF16, name="Bg", tag="xg", align_bytes=256)
         Bg32 = Bg[:].bitcast(F32)
-        for j in range(4):
-            bk = bank()
-            if WARMB and j:
-                warm_up(WARMB)
-                bk = bank()
-            t_rowtile(bk, Bsb[:].bitcast(F32), j * 512)
-            c_rowtile(bk, Bg32[:, j * 512 : (j + 1) * 512].rearrange("p (g n u) -> p g n u", g=2, u=2))
-        emit_Q(0)
-        for hf in range(2):
+
+        def quant_B(a, b):
             nc.vector.quantize_mx(
-                out=Bq[:, hf * 512 : (hf + 1) * 512].bitcast(FP8X4),
-                scales=Bs[:, hf * 512 : (hf + 1) * 512],
-                in_=Bg[:, hf * 2048 : (hf + 1) * 2048],
+                out=Bq[:, a * 256 : b * 256].bitcast(FP8X4), scales=Bs[:, a * 256 : b * 256], in_=Bg[:, a * 1024 : b * 1024]
             )
-        if X_LATE:
-            parts[1][8]()
-            if not TRIP1:
+
+        for tok in HEAD:
+            if tok == "gates":
+                for n in range(8):
+                    parts[0][n]()
+                    parts[1][n]()
+                parts[0][8]()
+            elif tok == "G":
+                parts[1][8]()
+            elif tok == "X":
+                for k in range(4):
+                    emit_X(k)
+            elif tok == "X45":
                 emit_X(4)
                 emit_X(5)
+            elif tok == "T0":
+                emit_T(0)
+            elif tok == "Q0":
+                emit_Q(0)
+            elif tok == "T1":
+                emit_T(1)
+            elif tok == "Q1":
+                emit_Q(1)
+            elif tok[0] == "L":
+                late_steps[int(tok[1])]()
+            elif tok[0:2] == "QB":
+                quant_B(int(tok[2]), int(tok[3]))
+            elif tok == "w":
+                warm_up(WARMB)
+            else:
+                j = int(tok[1])
+                bk = bank()
+                t_rowtile(bk, Bsb[:].bitcast(F32), j * 512)
+                dst = Bg32[:, j * 512 : (j + 1) * 512].rearrange("p (g n u) -> p g n u", g=2, u=2)
+                if tok[0] == "B":
+                    c_rowtile(bk, dst)
+                else:
+                    nc.vector.tensor_copy(out=dst, in_=bk[:].rearrange("p (g u n) -> p g n u", g=2, u=2))
 
         wag = {}
 
@@ -431,9 +480,14 @@ def tile_submatrixlinear_pa_t_kernel(tc, x, scores, Wb, bb, A, B, out):
             WAg32 = wag["t"][:].bitcast(F32)
             bk = bank()
             if what == "W0" or what == "W1":
-                h = 0 if what == "W0" else 1
-                t_rowtile(bk, Wsb[:].bitcast(F32), h * 512)
-                c_rowtile(bk, WAg32[:, 0:1024].rearrange("p (g h n u) -> p g h n u", g=2, h=2, u=2)[:, :, h])
+                g = 0 if what == "W0" else 1
+                for c in range(4):
+                    w0 = (c % 2) * 512 + g * 256 + (c // 2) * P
+                    nc.tensor.transpose(bk[:, c * P : (c + 1) * P], Wsb[:].bitcast(F32)[:, w0 : w0 + P], ident[:])
+                nc.scalar.copy(
+                    out=WAg32[:, g * 512 : (g + 1) * 512].rearrange("p (n h u) -> p n h u", h=2, u=2),
+                    in_=bk[:].rearrange("p (u h n) -> p n h u", u=2, h=2),
+                )
             elif what == "A":
                 for c in range(4):
                     nc.tensor.transpose(bk[:, c * P : (c + 1) * P], Ar[:, c * P : (c + 1) * P], ident[:])
@@ -470,8 +524,8 @@ def tile_submatrixlinear_pa_t_kernel(tc, x, scores, Wb, bb, A, B, out):
                 emit_trip()
             for k in BUNCH.get(i, []):
                 emit_T(k)
-            if i == -1:
-                warm_up(WARMB)
+            if TRIP_Q == "scalar" and i == READ_AT:
+                emit_trip_read()
             for k in GATE_T.get(i, []):
                 if not (TRIP1 and GROUPS[k][0] >= 8):
                     emit_Tg(k)
@@ -488,14 +542,24 @@ def tile_submatrixlinear_pa_t_kernel(tc, x, scores, Wb, bb, A, B, out):
                         emit_Hq(i)
                 if n < no:
                     emit_O(*o_pairs.pop(0))
+                if i in Q_MID and n == 0:
+                    for k in BUNCH.get(i, []):
+                        emit_Q(k)
                 if i in LATE_MID and n == 0:
                     late_gate_steps(LATE_MID[i][0], LATE_MID[i][1])
             for k in BUNCH.get(i, []):
-                emit_Q(k)
+                if i not in Q_MID:
+                    emit_Q(k)
             if 0 <= i < ng and not (HQE and i == ng - 1):
                 emit_Hq(i)
             if i in LATE_END:
                 late_gate_steps(LATE_END[i][0], LATE_END[i][1])
+            if PE_TILES == 24 and i == X67_AT:
+                emit_X(6)
+                emit_X(7)
+            if i == X45_AT:
+                emit_X(4)
+                emit_X(5)
             if i == ORDER_AT:
                 order_A()
             for what in PREP.get(i, []):

@@ -14,7 +14,7 @@ AX = mybir.AxisListType
 
 P = 128
 NT = 32
-HALF = 16
+HALF = 32
 FLOPS = 2 * 4096 * 1024 * 768 + 2 * 4096 * 512 * 256
 
 GROUPS = [(0, 2), (2, 2), (4, 2), (6, 2), (8, 4), (12, 4), (16, 4), (20, 4), (24, 4), (28, 2), (30, 2)]
@@ -40,6 +40,11 @@ UFIRST = []
 TRIP_Q = "sync"
 PE_TILES = 16
 Q_MID = []
+Q_AT = {}
+XG_BUFS = 3
+H_BUFS = 2
+HW_BUFS = 2
+OB_BUFS = 8
 X45_AT = -9
 HEAD = ["gates", "L0", "L1", "X", "T0", "B0", "B1", "B2", "B3", "Q0", "QB02", "QB24", "G", "X45"]
 SPLIT = []
@@ -59,12 +64,12 @@ def tile_submatrixlinear_pa_t_kernel(tc, x, scores, Wb, bb, A, B, out):
     with ExitStack() as ctx:
         const = ctx.enter_context(tc.tile_pool(name="const", bufs=1))
         xin_pool = ctx.enter_context(tc.tile_pool(name="xin", bufs=1))
-        xg_pool = ctx.enter_context(tc.tile_pool(name="xg", bufs=3))
+        xg_pool = ctx.enter_context(tc.tile_pool(name="xg", bufs=XG_BUFS))
         xq_pool = ctx.enter_context(tc.tile_pool(name="xq", bufs=XQ_BUFS))
-        h_pool = ctx.enter_context(tc.tile_pool(name="h", bufs=2))
-        hw_pool = ctx.enter_context(tc.tile_pool(name="hw", bufs=2))
+        h_pool = ctx.enter_context(tc.tile_pool(name="h", bufs=H_BUFS))
+        hw_pool = ctx.enter_context(tc.tile_pool(name="hw", bufs=HW_BUFS))
         hq_pool = ctx.enter_context(tc.tile_pool(name="hq", bufs=HQ_BUFS))
-        ob_pool = ctx.enter_context(tc.tile_pool(name="ob", bufs=8))
+        ob_pool = ctx.enter_context(tc.tile_pool(name="ob", bufs=OB_BUFS))
         psum = ctx.enter_context(tc.psum_pool(name="psum", bufs=1))
         ctx.enter_context(tc.manual_schedule())
 
@@ -121,7 +126,7 @@ def tile_submatrixlinear_pa_t_kernel(tc, x, scores, Wb, bb, A, B, out):
         def load(item):
             if item == "sc":
                 nc.sync.dma_start(
-                    out=sc[:].rearrange("p (h w) -> p h w", h=2), in_=scores.rearrange("(h p t) k -> p h (t k)", p=P, t=HALF)
+                    out=sc[:].rearrange("p (h w) -> p h w", h=NT // HALF), in_=scores.rearrange("(h p t) k -> p h (t k)", p=P, t=HALF)
                 )
             elif item == "B":
                 w = 4 // B_DMAS
@@ -548,7 +553,10 @@ def tile_submatrixlinear_pa_t_kernel(tc, x, scores, Wb, bb, A, B, out):
                 if i in LATE_MID and n == 0:
                     late_gate_steps(LATE_MID[i][0], LATE_MID[i][1])
             for k in BUNCH.get(i, []):
-                if i not in Q_MID:
+                if i not in Q_MID and k not in Q_AT:
+                    emit_Q(k)
+            for k in Q_AT:
+                if Q_AT[k] == i:
                     emit_Q(k)
             if 0 <= i < ng and not (HQE and i == ng - 1):
                 emit_Hq(i)

from contextlib import ExitStack

import concourse.mybir as mybir
from concourse.masks import make_identity

F32 = mybir.dt.float32
BF16 = mybir.dt.bfloat16
U32 = mybir.dt.uint32
U8 = mybir.dt.uint8
FP8X4 = mybir.dt.float8_e4m3fn_x4
ALU = mybir.AluOpType
ACT = mybir.ActivationFunctionType
AX = mybir.AxisListType

P = 128
NT = 32
HALF = 32
FLOPS = 2 * 4096 * 1024 * 768 + 2 * 4096 * 512 * 256

GROUPS = [(0, 2), (2, 2), (4, 2), (6, 2), (8, 4), (12, 4), (16, 4), (20, 4), (24, 4), (28, 2), (30, 2)]
LOADS = ["sc", (0, 2), "B", (2, 2), (4, 2), (6, 2), "W", "bb", (8, 4), (12, 4), "A", (16, 4), (20, 4)]
BUNCH = {-1: [1], 0: [2], 1: [3], 2: [4], 3: [5], 4: [6], 5: [7], 6: [8], 7: [9, 10]}
PREP = {1: ["W0"], 2: ["W1", "bias"], 3: ["A"]}
GATE_T = {-1: [0], 0: [1], 1: [2, 3, 4, 5]}
LATE_MID = {0: (3, 5), 1: (6, 7)}
LATE_END = {-1: (2, 3), 0: (5, 6), 1: (7, 9)}
TRIP_AT = 3
TRIP1 = False
WIDE = [4, 5, 6, 7, 8, 9]
O_PAIRS = {4: 1, 5: 1, 6: 1, 7: 1, 8: 3, 9: 3, 10: 2}
OFFLOAD = [(4, 0), (5, 0), (6, 0)]
X_LATE = False
ORDER_A = "scalar"
ORDER_AT = 2
O_SPLIT_LAST = 0
XQ_BUFS = 7
HQ_BUFS = 6
B_DMAS = 2
UFIRST = []
TRIP_Q = "sync"
PE_TILES = 16
Q_MID = []
Q_AT = {}
XG_BUFS = 3
H_BUFS = 2
HW_BUFS = 2
OB_BUFS = 8
X45_AT = -9
HEAD = ["gates", "L0", "L1", "X", "T0", "B0", "B1", "B2", "B3", "Q0", "QB02", "QB24", "G", "X45"]
SPLIT = []
CHUNK = 1
TRIP_MID = [24]
TRIP_END = [28]
X67_AT = 2
READ_AT = 4
HQE = False
WARM0 = 0
WARMB = 0


def tile_submatrixlinear_pa_t_kernel(tc, x, scores, Wb, bb, A, B, out):
    nc = tc.nc
    ng = len(GROUPS)
    with ExitStack() as ctx:
        const = ctx.enter_context(tc.tile_pool(name="const", bufs=1))
        xin_pool = ctx.enter_context(tc.tile_pool(name="xin", bufs=1))
        xg_pool = ctx.enter_context(tc.tile_pool(name="xg", bufs=XG_BUFS))
        xq_pool = ctx.enter_context(tc.tile_pool(name="xq", bufs=XQ_BUFS))
        h_pool = ctx.enter_context(tc.tile_pool(name="h", bufs=H_BUFS))
        hw_pool = ctx.enter_context(tc.tile_pool(name="hw", bufs=HW_BUFS))
        hq_pool = ctx.enter_context(tc.tile_pool(name="hq", bufs=HQ_BUFS))
        ob_pool = ctx.enter_context(tc.tile_pool(name="ob", bufs=OB_BUFS))
        psum = ctx.enter_context(tc.psum_pool(name="psum", bufs=1))
        ctx.enter_context(tc.manual_schedule())

        used = [0]

        def bank():
            b = used[0] % 8
            used[0] = used[0] + 1
            return psum.tile([P, 512], F32, name="bank%d" % b, tag="bank%d" % b)

        ident = const.tile([P, P], F32, name="ident")
        ones = const.tile([P, P], BF16, name="ones")
        bbz = const.tile([P, 256], BF16, name="bbz")
        bb2 = const.tile([P, 256], F32, name="bb2")
        warm = const.tile([P, 1], F32, name="warm")
        sc = const.tile([P, 512], BF16, name="sc")
        gT = const.tile([P, PE_TILES * P], F32, name="gT")
        gT2 = const.tile([P, (32 - PE_TILES) * P], F32, name="gT2")
        Ar = const.tile([P, 512], F32, name="Ar")
        gc = const.tile([P, (32 - PE_TILES) * 16], F32, name="gc")
        gc1 = const.tile([P, P], F32, name="gc1")
        Bsb = xin_pool.tile([P, 4096], BF16, name="Bsb", tag="xin7")
        Wsb = const.tile([P, 2048], BF16, name="Wsb")
        Asb = const.tile([P, 1024], BF16, name="Asb")
        Bq = const.tile([P, 1024], U32, name="Bq", align_bytes=256)
        Bs = const.tile([P, 1024], U8, name="Bs", align_bytes=256)
        Wq = const.tile([P, 512], U32, name="Wq", align_bytes=256)
        Ws = const.tile([P, 512], U8, name="Ws", align_bytes=256)
        Aq = const.tile([P, 256], U32, name="Aq", align_bytes=256)
        As = const.tile([P, 256], U8, name="As", align_bytes=256)
        xin = {}
        for i in range(7):
            xin[i] = xin_pool.tile([P, 4096], BF16, name="xin%d" % i, tag="xin%d" % i)

        nc.vector.memset(warm[:], 0.0)
        nc.vector.memset(bbz[:], 0.0)
        nc.vector.memset(ones[:], 1.0)
        make_identity(nc, ident[:])
        wz = const.tile([P, 512], BF16, name="wz")
        if WARM0:
            nc.gpsimd.memset(wz[:], 0.0)
        nc.scalar.activation(out=warm[:], in_=warm[:], func=ACT.Exp)

        x_v = x.rearrange("(h p t) i -> h p t i", p=P, t=HALF)
        out_v = out.rearrange("(h p t) o -> h p t o", p=P, t=HALF)
        B_v = B.rearrange("k r i -> (k r) i").rearrange("(p j) i -> p j i", j=4)

        def load_x(t0, cnt):
            if t0 == 28:
                xin[7] = xin_pool.tile([P, 4096], BF16, name="xin7", tag="xin7")
            dst = xin[t0 // 4][:, (t0 % 4) * 1024 : (t0 % 4 + cnt) * 1024]
            nc.sync.dma_start(out=dst.rearrange("p (t i) -> p t i", i=1024), in_=x_v[t0 // HALF, :, t0 % HALF : t0 % HALF + cnt, :])

        def load(item):
            if item == "sc":
                nc.sync.dma_start(
                    out=sc[:].rearrange("p (h w) -> p h w", h=NT // HALF), in_=scores.rearrange("(h p t) k -> p h (t k)", p=P, t=HALF)
                )
            elif item == "B":
                w = 4 // B_DMAS
                for j in range(0, 4, w):
                    nc.sync.dma_start(
                        out=Bsb[:, j * 1024 : (j + w) * 1024].rearrange("p (j i) -> p j i", i=1024), in_=B_v[:, j : j + w, :]
                    )
            elif item == "W":
                nc.sync.dma_start(out=Wsb[:], in_=Wb.rearrange("(p h) i -> p (h i)", h=2))
            elif item == "A":
                nc.sync.dma_start(
                    out=Asb[:].rearrange("p (k c) -> p k c", c=64), in_=A.rearrange("k (p h) r -> p k (h r)", h=2)
                )
            elif item == "bb":
                nc.sync.dma_start(out=bbz[0:1, :], in_=bb.rearrange("(o n) -> o n", o=1))
            else:
                load_x(item[0], item[1])

        for item in LOADS:
            load(item)

        def t_rowtile(bk, src32, col0):
            for c in range(4):
                nc.tensor.transpose(bk[:, c * P : (c + 1) * P], src32[:, col0 + c * P : col0 + (c + 1) * P], ident[:])

        def c_rowtile(bk, dst):
            nc.scalar.copy(out=dst, in_=bk[:].rearrange("p (g u n) -> p g n u", g=2, u=2))

        gsrc = {}
        gexps = {}

        def emit_X(k):
            t0, cnt = GROUPS[k]
            ge = const.tile([P, cnt * P], F32, name="ge%d" % k)
            gg, c0 = gsrc[t0]
            nc.gpsimd.tensor_scalar(
                out=ge[:].rearrange("p (c r) -> p c r", r=8),
                in0=gg[:, c0 : c0 + cnt * 16].unsqueeze(2).to_broadcast([P, cnt * 16, 8]),
                scalar1=1.0, scalar2=0.0, op0=ALU.mult, op1=ALU.add,
            )
            gexps[k] = ge

        def gate_steps(part, ta, tb):
            n = tb - ta
            w = n * 16
            s3 = sc[:, ta * 16 : tb * 16].rearrange("p (t k) -> p t k", k=16)
            mx = const.tile([P, n], F32, name="mx%d" % part)
            dd = const.tile([P, w], F32, name="dd%d" % part)
            ee = const.tile([P, w], F32, name="ee%d" % part)
            ss = const.tile([P, n], F32, name="ss%d" % part)
            g0 = const.tile([P, w], F32, name="g0%d" % part)
            g1 = const.tile([P, w], F32, name="g1%d" % part)
            s1 = const.tile([P, n], F32, name="s1%d" % part)
            r1 = const.tile([P, n], F32, name="r1%d" % part)
            gg = const.tile([P, w], F32, name="gg%d" % part)

            def v3(t):
                return t[:].rearrange("p (t k) -> p t k", k=16)

            def b3(t):
                return t[:].unsqueeze(2).to_broadcast([P, n, 16])

            def st_max():
                nc.vector.tensor_reduce(out=mx[:], in_=s3, axis=AX.X, op=ALU.max)

            def st_sub():
                nc.vector.tensor_tensor(out=v3(dd), in0=s3, in1=b3(mx), op=ALU.subtract)

            def st_exp():
                nc.scalar.activation(out=ee[:], in_=dd[:], func=ACT.Exp)

            def st_sum():
                nc.vector.tensor_reduce(out=ss[:], in_=v3(ee), axis=AX.X, op=ALU.add)

            def st_g0():
                nc.vector.scalar_tensor_tensor(out=v3(g0), in0=v3(ee), scalar=20.0, in1=b3(ss), op0=ALU.mult, op1=ALU.is_gt)

            def st_thr():
                nc.vector.tensor_tensor(out=g1[:], in0=g0[:], in1=ee[:], op=ALU.mult)

            def st_sum1():
                nc.vector.tensor_reduce(out=s1[:], in_=v3(g1), axis=AX.X, op=ALU.add)

            def st_rec():
                nc.vector.reciprocal(out=r1[:], in_=s1[:])

            def st_g():
                nc.vector.tensor_tensor(out=v3(gg), in0=v3(g1), in1=b3(r1), op=ALU.mult)

            for t in range(ta, tb):
                gsrc[t] = (gg, (t - ta) * 16)
            return [st_max, st_sub, st_exp, st_sum, st_g0, st_thr, st_sum1, st_rec, st_g]

        xgs = {}
        xqs = {}
        hgs = {}
        hqs = {}
        late_stores = []

        def emit_T(k):
            t0, cnt = GROUPS[k]
            xg = xg_pool.tile([P, 4096], BF16, name="xg", tag="xg", align_bytes=256)
            xg32 = xg[:].bitcast(F32)
            for tt in range(cnt):
                t = t0 + tt
                bk = bank()
                t_rowtile(bk, xin[t // 4][:].bitcast(F32), (t % 4) * 512)
                pair = xg32[:, (tt // 2) * 1024 : (tt // 2 + 1) * 1024].rearrange("p (g t n u) -> p g t n u", g=2, t=2, u=2)
                c_rowtile(bk, pair[:, :, tt % 2])
            xgs[k] = xg

        def emit_Tg(k):
            t0, cnt = GROUPS[k]
            bk = bank()
            for tt in range(cnt):
                nc.tensor.transpose(bk[:, tt * P : (tt + 1) * P], gexps[k][:, tt * P : (tt + 1) * P], ident[:])
            nc.scalar.copy(out=gT[:, t0 * P : (t0 + cnt) * P], in_=bk[:, 0 : cnt * P])

        def emit_trip_read():
            q = nc.scalar if TRIP_Q == "scalar" else nc.sync
            q.dma_start(
                out=gT2[:].rearrange("p (t n) -> p t n", t=8), in_=out[3072:4096, 0 : (32 - PE_TILES) * 16].rearrange("(t q) n -> q t n", q=P)
            )

        def emit_trip():
            bk = bank()
            nb = (32 - PE_TILES) // 8
            for c in range(nb):
                c0 = (PE_TILES - 16) * 16 + c * P
                nc.tensor.transpose(bk[:, c * P : (c + 1) * P], gsrc[16][0][:, c0 : c0 + P], ident[:])
            nc.scalar.copy(out=gc[:], in_=bk[:, 0 : nb * P])
            q = nc.scalar if TRIP_Q == "scalar" else nc.sync
            q.dma_start(
                out=out[3072:4096, 0 : (32 - PE_TILES) * 16].rearrange("(q r) n -> q r n", r=8), in_=gc[:].unsqueeze(1).to_broadcast([P, 8, (32 - PE_TILES) * 16])
            )
            if TRIP_Q == "sync":
                for t0 in TRIP_MID:
                    load_x(t0, 4)
                emit_trip_read()
                for t0 in TRIP_END:
                    load_x(t0, 4)
            else:
                load_x(28, 4)

        def emit_trip1():
            bk = bank()
            nc.tensor.transpose(bk[:, 0:P], gsrc[8][0][:], ident[:])
            nc.scalar.copy(out=gc1[:], in_=bk[:, 0:P])
            scratch = out[2048:3072, 0:P]
            nc.sync.dma_start(
                out=scratch.rearrange("(q r) n -> q r n", r=8), in_=gc1[:].unsqueeze(1).to_broadcast([P, 8, P])
            )
            load_x(12, 4)
            nc.sync.dma_start(
                out=gT[:, 8 * P : 16 * P].rearrange("p (t n) -> p t n", n=P), in_=scratch.rearrange("(t q) n -> q t n", q=P)
            )
            load("A")
            load_x(16, 4)
            load_x(20, 4)

        def emit_Q(k):
            t0, cnt = GROUPS[k]
            xq = xq_pool.tile([P, 1024], U32, name="xq", tag="xq", align_bytes=256)
            xs = xq_pool.tile([P, 1024], U8, name="xs", tag="xs", align_bytes=256)
            nc.vector.quantize_mx(
                out=xq[:, 0 : cnt * 256].bitcast(FP8X4), scales=xs[:, 0 : cnt * 256], in_=xgs[k][:, 0 : cnt * 1024]
            )
            xqs[k] = (xq, xs)

        def gate_pair(t):
            if t < PE_TILES:
                return gT[:, t * P : (t + 2) * P].rearrange("p (t n) -> p t n", t=2)
            v = gT2[:].rearrange("p (t c n) -> p c t n", t=8, n=P)
            return v[:, (t - PE_TILES) // 8, t % 8 : t % 8 + 2]

        def emit_U(k, p0):
            t0, cnt = GROUPS[k]
            xq, xs = xqs[k]
            if p0 == 0:
                hgs[k] = h_pool.tile([P, 2048], BF16, name="hg", tag="hg", align_bytes=256)
            hg = hgs[k]
            if k not in WIDE:
                for tt in range(p0, p0 + 2):
                    bk = bank()
                    for j in range(4):
                        for g in range(2):
                            wc = slice((j * 2 + g) * P, (j * 2 + g + 1) * P)
                            c0 = p0 * 256 + g * 256 + (tt - p0) * P
                            nc.tensor.matmul_mx(
                                out=bk[:, j * P : (j + 1) * P],
                                lhsT=Bq[:, wc].bitcast(FP8X4), lhsT_scale=Bs[:, wc],
                                rhs=xq[:, c0 : c0 + P].bitcast(FP8X4), rhs_scale=xs[:, c0 : c0 + P],
                                start=(g == 0), stop=(g == 1),
                            )
                    nc.vector.tensor_tensor(
                        out=hg[:, tt * 512 : (tt + 1) * 512].rearrange("p (n j) -> p n j", j=4),
                        in0=bk[:].rearrange("p (j n) -> p n j", j=4),
                        in1=gate_pair(t0 + p0)[:, tt - p0].unsqueeze(2).to_broadcast([P, P, 4]),
                        op=ALU.mult,
                    )
                return
            hw = hw_pool.tile([P, 1024], BF16, name="hw", tag="hw", align_bytes=256)
            for u in range(2):
                bk = bank()
                for e in range(2):
                    for g in range(2):
                        wc = slice(((2 * u + e) * 2 + g) * P, ((2 * u + e) * 2 + g + 1) * P)
                        xc = slice(p0 * 256 + g * 256, p0 * 256 + (g + 1) * 256)
                        nc.tensor.matmul_mx(
                            out=bk[:, e * 256 : (e + 1) * 256],
                            lhsT=Bq[:, wc].bitcast(FP8X4), lhsT_scale=Bs[:, wc],
                            rhs=xq[:, xc].bitcast(FP8X4), rhs_scale=xs[:, xc],
                            start=(g == 0), stop=(g == 1),
                        )
                nc.vector.tensor_tensor(
                    out=hw[:, u * 512 : (u + 1) * 512].rearrange("p (t n e) -> p t n e", t=2, e=2),
                    in0=bk[:].rearrange("p (e t n) -> p t n e", e=2, t=2),
                    in1=gate_pair(t0 + p0).unsqueeze(3).to_broadcast([P, 2, P, 2]),
                    op=ALU.mult,
                )
            nc.scalar.copy(
                out=hg[:, p0 * 512 : (p0 + 2) * 512].bitcast(F32).rearrange("p (n u) -> p n u", u=2),
                in_=hw[:].bitcast(F32).rearrange("p (u n) -> p n u", u=2),
            )

        def emit_Hq(k):
            t0, cnt = GROUPS[k]
            hq = hq_pool.tile([P, 512], U32, name="hq", tag="hq", align_bytes=256)
            hs = hq_pool.tile([P, 512], U8, name="hs", tag="hs", align_bytes=256)
            nc.vector.quantize_mx(
                out=hq[:, 0 : cnt * P].bitcast(FP8X4), scales=hs[:, 0 : cnt * P], in_=hgs[k][:, 0 : cnt * 512]
            )
            hqs[k] = (hq, hs)

        def emit_O(k, p0):
            t0, cnt = GROUPS[k]
            xq, xs = xqs[k]
            hq, hs = hqs[k]
            split = (k, p0) in SPLIT
            bk = bank()
            bks = [bk, bank()] if split else [bk, bk]
            for q in range(2):
                bk = bks[q]
                oc = slice(0, 256) if split else slice(q * 256, (q + 1) * 256)
                for g in range(2):
                    c0 = p0 * 256 + g * 256 + q * P
                    nc.tensor.matmul_mx(
                        out=bk[:, oc],
                        lhsT=xq[:, c0 : c0 + P].bitcast(FP8X4), lhsT_scale=xs[:, c0 : c0 + P],
                        rhs=Wq[:, g * 256 : (g + 1) * 256].bitcast(FP8X4), rhs_scale=Ws[:, g * 256 : (g + 1) * 256],
                        start=(g == 0), stop=False,
                    )
                hc = slice((p0 + q) * P, (p0 + q + 1) * P)
                nc.tensor.matmul_mx(
                    out=bk[:, oc],
                    lhsT=hq[:, hc].bitcast(FP8X4), lhsT_scale=hs[:, hc],
                    rhs=Aq[:].bitcast(FP8X4), rhs_scale=As[:],
                    start=False, stop=True,
                )
                if split:
                    ob = ob_pool.tile([P, 512], F32, name="ob", tag="ob")
                    nc.vector.tensor_tensor(out=ob[:, 0:256], in0=bk[:, 0:256], in1=bb2[:], op=ALU.add)
                    t = t0 + p0 + q
                    nc.sync.dma_start(out=out_v[t // HALF, :, t % HALF, :], in_=ob[:, 0:256])
            if split:
                return
            ob = ob_pool.tile([P, 512], F32, name="ob", tag="ob")
            o3 = ob[:].rearrange("p (t o) -> p t o", o=256)
            b3 = bb2[:].unsqueeze(1).to_broadcast([P, 2, 256])
            t = t0 + p0
            dram = out_v[t // HALF, :, t % HALF : t % HALF + 2, :]

            def store():
                nc.sync.dma_start(out=dram, in_=o3)

            if (k, p0) in OFFLOAD:
                nc.scalar.copy(out=ob[:], in_=bk[:])
                w = 512 // CHUNK
                for c in range(0, 512, w):
                    if w > 256:
                        nc.gpsimd.tensor_tensor(out=o3, in0=o3, in1=b3, op=ALU.add)
                    else:
                        nc.gpsimd.tensor_tensor(out=ob[:, c : c + w], in0=ob[:, c : c + w], in1=bb2[:, c % 256 : c % 256 + w], op=ALU.add)
                late_stores.append(store)
            else:
                nc.vector.tensor_tensor(out=o3, in0=bk[:].rearrange("p (t o) -> p t o", o=256), in1=b3, op=ALU.add)
                store()
                while late_stores:
                    late_stores.pop(0)()

        parts = [gate_steps(n, ta, tb) for n, (ta, tb) in enumerate([(0, 8), (8, 16), (16, 32)])]
        late_steps = parts[2]

        def late_gate_steps(a, b):
            for f in late_steps[a:b]:
                f()

        def warm_up(n):
            if n:
                bk = bank()
                for m in range(n):
                    nc.tensor.matmul(out=bk[:], lhsT=wz[:, 0:P], rhs=wz[:], start=True, stop=True)

        warm_up(WARM0)
        Bg = xg_pool.tile([P, 4096], BF16, name="Bg", tag="xg", align_bytes=256)
        Bg32 = Bg[:].bitcast(F32)

        def quant_B(a, b):
            nc.vector.quantize_mx(
                out=Bq[:, a * 256 : b * 256].bitcast(FP8X4), scales=Bs[:, a * 256 : b * 256], in_=Bg[:, a * 1024 : b * 1024]
            )

        for tok in HEAD:
            if tok == "gates":
                for n in range(8):
                    parts[0][n]()
                    parts[1][n]()
                parts[0][8]()
            elif tok == "G":
                parts[1][8]()
            elif tok == "X":
                for k in range(4):
                    emit_X(k)
            elif tok == "X45":
                emit_X(4)
                emit_X(5)
            elif tok == "T0":
                emit_T(0)
            elif tok == "Q0":
                emit_Q(0)
            elif tok == "T1":
                emit_T(1)
            elif tok == "Q1":
                emit_Q(1)
            elif tok[0] == "L":
                late_steps[int(tok[1])]()
            elif tok[0:2] == "QB":
                quant_B(int(tok[2]), int(tok[3]))
            elif tok == "w":
                warm_up(WARMB)
            else:
                j = int(tok[1])
                bk = bank()
                t_rowtile(bk, Bsb[:].bitcast(F32), j * 512)
                dst = Bg32[:, j * 512 : (j + 1) * 512].rearrange("p (g n u) -> p g n u", g=2, u=2)
                if tok[0] == "B":
                    c_rowtile(bk, dst)
                else:
                    nc.vector.tensor_copy(out=dst, in_=bk[:].rearrange("p (g u n) -> p g n u", g=2, u=2))

        wag = {}

        def prep_piece(what):
            if "t" not in wag:
                wag["t"] = xg_pool.tile([P, 3072], BF16, name="WAg", tag="wag", bufs=1, align_bytes=256)
            WAg32 = wag["t"][:].bitcast(F32)
            bk = bank()
            if what == "W0" or what == "W1":
                g = 0 if what == "W0" else 1
                for c in range(4):
                    w0 = (c % 2) * 512 + g * 256 + (c // 2) * P
                    nc.tensor.transpose(bk[:, c * P : (c + 1) * P], Wsb[:].bitcast(F32)[:, w0 : w0 + P], ident[:])
                nc.scalar.copy(
                    out=WAg32[:, g * 512 : (g + 1) * 512].rearrange("p (n h u) -> p n h u", h=2, u=2),
                    in_=bk[:].rearrange("p (u h n) -> p n h u", u=2, h=2),
                )
            elif what == "A":
                for c in range(4):
                    nc.tensor.transpose(bk[:, c * P : (c + 1) * P], Ar[:, c * P : (c + 1) * P], ident[:])
                nc.scalar.copy(
                    out=WAg32[:, 1024:1536].rearrange("p (n h u) -> p n h u", h=2, u=2),
                    in_=bk[:].rearrange("p (u h n) -> p n h u", u=2, h=2),
                )
            else:
                nc.tensor.matmul(out=bk[:, 0:256], lhsT=ones[:], rhs=bbz[:], start=True, stop=True)
                nc.scalar.copy(out=bb2[:], in_=bk[:, 0:256])

        def order_A():
            A5 = Asb[:].bitcast(F32).rearrange("p (k h m u) -> p u h k m", h=2, m=8, u=2)
            for u in range(2):
                dst = Ar[:, u * 256 : (u + 1) * 256].rearrange("p (h k m) -> p h k m", h=2, m=8)
                if ORDER_A == "scalar":
                    nc.scalar.copy(out=dst, in_=A5[:, u])
                else:
                    nc.vector.tensor_copy(out=dst, in_=A5[:, u])

        def quant_piece(what):
            WAg = wag["t"]
            if what == "W1":
                nc.vector.quantize_mx(out=Wq[:].bitcast(FP8X4), scales=Ws[:], in_=WAg[:, 0:2048])
            if what == "A":
                nc.vector.quantize_mx(out=Aq[:].bitcast(FP8X4), scales=As[:], in_=WAg[:, 2048:3072])

        o_pairs = [(k, p0) for k in range(ng) for p0 in range(0, GROUPS[k][1], 2)]
        for i in range(-1, ng + 1):
            if i in UFIRST:
                for p0 in range(0, GROUPS[i][1], 2):
                    emit_U(i, p0)
            if i == TRIP_AT:
                emit_trip()
            for k in BUNCH.get(i, []):
                emit_T(k)
            if TRIP_Q == "scalar" and i == READ_AT:
                emit_trip_read()
            for k in GATE_T.get(i, []):
                if not (TRIP1 and GROUPS[k][0] >= 8):
                    emit_Tg(k)
            if TRIP1 and i == 0:
                emit_trip1()
            for what in PREP.get(i, []):
                prep_piece(what)
            nu = GROUPS[i][1] // 2 if 0 <= i < ng and i not in UFIRST else 0
            no = len(o_pairs) if i >= ng else O_PAIRS.get(i, 0)
            for n in range(max(nu, no)):
                if n < nu:
                    emit_U(i, 2 * n)
                    if i == ng - 1 and HQE:
                        emit_Hq(i)
                if n < no:
                    emit_O(*o_pairs.pop(0))
                if i in Q_MID and n == 0:
                    for k in BUNCH.get(i, []):
                        emit_Q(k)
                if i in LATE_MID and n == 0:
                    late_gate_steps(LATE_MID[i][0], LATE_MID[i][1])
            for k in BUNCH.get(i, []):
                if i not in Q_MID and k not in Q_AT:
                    emit_Q(k)
            for k in Q_AT:
                if Q_AT[k] == i:
                    emit_Q(k)
            if 0 <= i < ng and not (HQE and i == ng - 1):
                emit_Hq(i)
            if i in LATE_END:
                late_gate_steps(LATE_END[i][0], LATE_END[i][1])
            if PE_TILES == 24 and i == X67_AT:
                emit_X(6)
                emit_X(7)
            if i == X45_AT:
                emit_X(4)
                emit_X(5)
            if i == ORDER_AT:
                order_A()
            for what in PREP.get(i, []):
                quant_piece(what)
        while late_stores:
            late_stores.pop(0)()
